import numpy as np
import ml_dtypes

BF16 = ml_dtypes.bfloat16


def bf(x):
    return np.asarray(x, np.float32).astype(BF16)


def f32(x):
    return np.asarray(x, np.float32)


def f64(x):
    return np.asarray(x).astype(np.float64)


def striped(idx):
    return np.tile(idx.reshape(-1, 16).T, (8, 1))


C, S, N, P, A = 128, 256, 512, 4, 2
EPS = 1e-6
LOGIT_SCALE = 6.0
POLY_SCALE = 0.3


def setup_inputs():
    return {"logits": f32(LOGIT_SCALE * np.random.standard_normal((C, S))), "pred_poly": f32(POLY_SCALE * np.random.standard_normal((C, P * A))), "tgt_poly": f32(POLY_SCALE * np.random.standard_normal((P * A, N))), "offs": striped(np.random.permutation(np.tile(np.arange(S), 2))[:N])}


def reference(logits, pred_poly, tgt_poly, offs):
    idx = offs[:16].T.reshape(-1)
    z = f64(logits)
    e = np.exp(z - z.max(axis=1, keepdims=True))
    prob = e / e.sum(axis=1, keepdims=True)
    x = f64(pred_poly).reshape(C, P, A)
    y = f64(tgt_poly).reshape(P, A, N)
    d = np.abs(x[:, :, None, :, None] - y[None, None, :, :, :]).sum(axis=3)
    chamfer = 0.5 * (d.min(axis=2).mean(axis=1) + d.min(axis=1).mean(axis=1))
    u = x[:, -1, :] - x[:, 0, :]
    un = u / (np.sqrt((u * u).sum(axis=1, keepdims=True)) + EPS)
    v = y[-1] - y[0]
    vn = v / (np.sqrt((v * v).sum(axis=0, keepdims=True)) + EPS)
    cosine = un @ vn
    return chamfer + 1.0 - cosine - prob[:, idx]

@@ -1,0 +1,134 @@
+import concourse.mybir as mybir
+from concourse.masks import make_identity
+
+F32 = mybir.dt.float32
+U16 = mybir.dt.uint16
+ALU = mybir.AluOpType
+FUNC = mybir.ActivationFunctionType
+FREE = mybir.AxisListType.X
+
+PREDS = 128
+CLASSES = 256
+TARGETS = 512
+POINTS = 4
+COORDS = 2
+EPS = 1e-6
+PIECE = 256
+BLOCK = 128
+N_BLOCKS = TARGETS // BLOCK
+
+FLOPS = PREDS * TARGETS * 118
+
+
+def tile_hungarianmatcher_kernel(tc, logits, pred_poly, tgt_poly, offs, out):
+    nc = tc.nc
+    with (
+        tc.tile_pool(name="held", bufs=1) as held,
+        tc.tile_pool(name="work", bufs=3) as work,
+        tc.psum_pool(name="psum", bufs=1) as psum,
+        tc.psum_pool(name="sums", bufs=2) as sums,
+    ):
+        offsets = held.tile([PREDS, TARGETS // 16], U16, name="offsets")
+        nc.sync.dma_start(offsets[:], offs)
+        x = held.tile([PREDS, POINTS * COORDS], F32, name="x")
+        nc.sync.dma_start(x[:], pred_poly)
+        y_all = held.tile([PREDS, COORDS, POINTS, TARGETS], F32, name="y_all")
+        for a in range(COORDS):
+            for q in range(POINTS):
+                queue = nc.sync if q % 2 == 0 else nc.scalar
+                row = tgt_poly[COORDS * q + a, :]
+                queue.dma_start(y_all[:, a, q, :], row.partition_broadcast(PREDS))
+        logit = held.tile([PREDS, CLASSES], F32, name="logit")
+        nc.scalar.dma_start(logit[:], logits)
+        y_rows = held.tile([POINTS * COORDS, TARGETS], F32, name="y_rows")
+        nc.gpsimd.dma_start(y_rows[:], tgt_poly)
+
+        ident = held.tile([PREDS, PREDS], F32, name="ident")
+        make_identity(nc, ident[:])
+        eighth = held.tile([PREDS, PREDS], F32, name="eighth")
+        nc.vector.tensor_scalar_mul(eighth[:], ident[:], 1.0 / (2 * POINTS))
+        halves = held.tile([PREDS, 1 + N_BLOCKS], F32, name="halves")
+        nc.gpsimd.memset(halves[:], 0.5)
+
+        top = held.tile([PREDS, 1], F32, name="top")
+        nc.vector.reduce_max(top[:], logit[:], axis=FREE)
+        neg_top = held.tile([PREDS, 1], F32, name="neg_top")
+        nc.vector.tensor_scalar_mul(neg_top[:], top[:], -1.0)
+        expd = held.tile([PREDS, CLASSES], F32, name="expd")
+        total = held.tile([PREDS, 1], F32, name="total")
+        nc.scalar.activation(expd[:], logit[:], FUNC.Exp, bias=neg_top[:], scale=1.0, accum_out=total[:])
+        inv_total = held.tile([PREDS, 1], F32, name="inv_total")
+        nc.vector.reciprocal(inv_total[:], total[:])
+        neg_prob = held.tile([PREDS, CLASSES], F32, name="neg_prob")
+        nc.vector.tensor_scalar(neg_prob[:], expd[:], inv_total[:], -1.0, ALU.mult, ALU.mult)
+
+        last_minus_first = held.tile([POINTS * COORDS, COORDS], F32, name="last_minus_first")
+        nc.vector.tensor_sub(
+            last_minus_first[:],
+            ident[0 : POINTS * COORDS, (POINTS - 1) * COORDS : POINTS * COORDS],
+            ident[0 : POINTS * COORDS, 0:COORDS],
+        )
+        v_ps = psum.tile([BLOCK, N_BLOCKS, COORDS], F32, name="v_ps")
+        for b in range(N_BLOCKS):
+            nc.tensor.matmul(
+                v_ps[:, b, :], y_rows[:, b * BLOCK : (b + 1) * BLOCK], last_minus_first[:], start=True, stop=True
+            )
+        dirs = held.tile([PREDS, 1 + N_BLOCKS, COORDS], F32, name="dirs")
+        nc.vector.tensor_sub(dirs[:, 0, :], x[:, (POINTS - 1) * COORDS : POINTS * COORDS], x[:, 0:COORDS])
+        nc.vector.tensor_copy(dirs[:, 1 : 1 + N_BLOCKS, :], v_ps[:])
+        squares = held.tile([PREDS, 1 + N_BLOCKS, COORDS], F32, name="squares")
+        nc.vector.tensor_mul(squares[:], dirs[:], dirs[:])
+        norm2 = held.tile([PREDS, 1 + N_BLOCKS], F32, name="norm2")
+        nc.vector.reduce_sum(norm2[:], squares[:], axis=FREE)
+        norm = held.tile([PREDS, 1 + N_BLOCKS], F32, name="norm")
+        nc.gpsimd.tensor_tensor(norm[:], norm2[:], halves[:], ALU.pow)
+        norm_eps = held.tile([PREDS, 1 + N_BLOCKS], F32, name="norm_eps")
+        nc.vector.tensor_scalar_add(norm_eps[:], norm[:], EPS)
+        inv_norm = held.tile([PREDS, 1 + N_BLOCKS], F32, name="inv_norm")
+        nc.vector.reciprocal(inv_norm[:], norm_eps[:])
+        unit = held.tile([PREDS, 1 + N_BLOCKS, COORDS], F32, name="unit")
+        nc.vector.tensor_mul(
+            unit[:], dirs[:], inv_norm[:].unsqueeze(2).to_broadcast([PREDS, 1 + N_BLOCKS, COORDS])
+        )
+        un_ps = psum.tile([COORDS, PREDS], F32, name="un_ps")
+        nc.tensor.transpose(un_ps[:], unit[:, 0, :], ident[:])
+        vn_ps = psum.tile([COORDS, TARGETS], F32, name="vn_ps")
+        for b in range(N_BLOCKS):
+            nc.tensor.transpose(vn_ps[:, b * BLOCK : (b + 1) * BLOCK], unit[:, 1 + b, :], ident[:])
+        neg_un = held.tile([COORDS, PREDS], F32, name="neg_un")
+        nc.vector.tensor_scalar_mul(neg_un[:], un_ps[:], -1.0)
+        vn = held.tile([COORDS, TARGETS], F32, name="vn")
+        nc.vector.tensor_copy(vn[:], vn_ps[:])
+
+        for piece in range(TARGETS // PIECE):
+            cols = slice(piece * PIECE, (piece + 1) * PIECE)
+            acc = sums.tile([PREDS, PIECE], F32, name="acc")
+            near_pred = work.tile([PREDS, POINTS, PIECE], F32, name="near_pred")
+            for p in range(POINTS):
+                gaps = work.tile([PREDS, COORDS, POINTS, PIECE], F32, name="gaps")
+                for a in range(COORDS):
+                    k = COORDS * p + a
+                    nc.scalar.activation(
+                        gaps[:, a], y_all[:, a, :, cols], FUNC.Abs, bias=x[:, k : k + 1], scale=-1.0
+                    )
+                if p == 0:
+                    dist = near_pred
+                else:
+                    dist = work.tile([PREDS, POINTS, PIECE], F32, name="dist")
+                nc.vector.tensor_tensor(dist[:], gaps[:, 0], gaps[:, 1], ALU.add)
+                pair = work.tile([PREDS, 2, PIECE], F32, name="pair")
+                nc.vector.tensor_tensor(pair[:], dist[:, 0:2], dist[:, 2:4], ALU.min)
+                near_tgt = work.tile([PREDS, PIECE], F32, name="near_tgt")
+                nc.vector.tensor_tensor(near_tgt[:], pair[:, 0], pair[:, 1], ALU.min)
+                nc.tensor.matmul(acc[:], eighth[:], near_tgt[:], start=(p == 0), stop=False)
+                if p > 0:
+                    nc.vector.tensor_tensor(near_pred[:], near_pred[:], dist[:], ALU.min)
+            nc.tensor.matmul(acc[:], neg_un[:], vn[:, cols], start=False, stop=False)
+            for q in range(POINTS):
+                nc.tensor.matmul(acc[:], eighth[:], near_pred[:, q], start=False, stop=(q == POINTS - 1))
+            rest = work.tile([PREDS, PIECE], F32, name="rest")
+            nc.vector.tensor_scalar_add(rest[:], acc[:], 1.0)
+            cost = work.tile([PREDS, PIECE], F32, name="cost")
+            picked = neg_prob[:].indirect(offsets[:, piece * (PIECE // 16) : (piece + 1) * (PIECE // 16)])
+            nc.vector.tensor_tensor(cost[:], picked, rest[:], ALU.add)
+            nc.sync.dma_start(out[:, cols], cost[:])

@@ -2,6 +2,7 @@ import concourse.mybir as mybir
 from concourse.masks import make_identity
 
 F32 = mybir.dt.float32
+BF16 = mybir.dt.bfloat16
 U16 = mybir.dt.uint16
 ALU = mybir.AluOpType
 FUNC = mybir.ActivationFunctionType
@@ -11,11 +12,13 @@ PREDS = 128
 CLASSES = 256
 TARGETS = 512
 POINTS = 4
+HALF = POINTS // 2
 COORDS = 2
 EPS = 1e-6
-PIECE = 256
-BLOCK = 128
-N_BLOCKS = TARGETS // BLOCK
+PIECE = 128
+N_PIECES = TARGETS // PIECE
+FOLD = TARGETS // PREDS
+N_DIRS = FOLD + 1
 
 FLOPS = PREDS * TARGETS * 118
 
@@ -24,31 +27,65 @@ def tile_hungarianmatcher_kernel(tc, logits, pred_poly, tgt_poly, offs, out):
     nc = tc.nc
     with (
         tc.tile_pool(name="held", bufs=1) as held,
-        tc.tile_pool(name="work", bufs=3) as work,
+        tc.tile_pool(name="gap_pool", bufs=3) as gap_pool,
+        tc.tile_pool(name="dist_pool", bufs=2) as dist_pool,
+        tc.tile_pool(name="min_pool", bufs=N_PIECES) as min_pool,
+        tc.tile_pool(name="out_pool", bufs=2) as out_pool,
         tc.psum_pool(name="psum", bufs=1) as psum,
-        tc.psum_pool(name="sums", bufs=2) as sums,
+        tc.psum_pool(name="sums", bufs=N_PIECES) as sums,
     ):
-        offsets = held.tile([PREDS, TARGETS // 16], U16, name="offsets")
-        nc.sync.dma_start(offsets[:], offs)
         x = held.tile([PREDS, POINTS * COORDS], F32, name="x")
         nc.sync.dma_start(x[:], pred_poly)
-        y_all = held.tile([PREDS, COORDS, POINTS, TARGETS], F32, name="y_all")
-        for a in range(COORDS):
-            for q in range(POINTS):
-                queue = nc.sync if q % 2 == 0 else nc.scalar
-                row = tgt_poly[COORDS * q + a, :]
-                queue.dma_start(y_all[:, a, q, :], row.partition_broadcast(PREDS))
+        ends = held.tile([PREDS, 2, COORDS, FOLD], F32, name="ends")
+        y_folded = tgt_poly.rearrange("(q a) (m i) -> q m a i", a=COORDS, i=FOLD)
+        nc.scalar.dma_start(ends[:, 0], y_folded[0])
+        nc.scalar.dma_start(ends[:, 1], y_folded[POINTS - 1])
+        y_all = held.tile([PREDS, N_PIECES, COORDS, POINTS, PIECE], F32, name="y_all")
+        y_by_coord = tgt_poly.rearrange("(q a) j -> a q j", a=COORDS)
         logit = held.tile([PREDS, CLASSES], F32, name="logit")
-        nc.scalar.dma_start(logit[:], logits)
-        y_rows = held.tile([POINTS * COORDS, TARGETS], F32, name="y_rows")
-        nc.gpsimd.dma_start(y_rows[:], tgt_poly)
+        for piece in range(N_PIECES):
+            cols = slice(piece * PIECE, (piece + 1) * PIECE)
+            for a, queue in enumerate((nc.sync, nc.scalar)):
+                source = y_by_coord[a, :, cols].unsqueeze(0).to_broadcast([PREDS, POINTS, PIECE])
+                queue.dma_start(y_all[:, piece, a], source)
+            if piece == 0:
+                nc.sync.dma_start(logit[:], logits)
+        offsets = held.tile([PREDS, TARGETS // 16], U16, name="offsets")
+        nc.sync.dma_start(offsets[:], offs)
 
         ident = held.tile([PREDS, PREDS], F32, name="ident")
         make_identity(nc, ident[:])
-        eighth = held.tile([PREDS, PREDS], F32, name="eighth")
+        root = held.tile([PREDS, N_DIRS], F32, name="root")
+        nc.gpsimd.memset(root[:], 0.5)
+        eighth = held.tile([PREDS, PREDS], BF16, name="eighth")
         nc.vector.tensor_scalar_mul(eighth[:], ident[:], 1.0 / (2 * POINTS))
-        halves = held.tile([PREDS, 1 + N_BLOCKS], F32, name="halves")
-        nc.gpsimd.memset(halves[:], 0.5)
+        warm = held.tile([PREDS, N_DIRS], F32, name="warm")
+        nc.scalar.activation(warm[:], root[:], FUNC.Exp)
+
+        dirs = held.tile([PREDS, COORDS, N_DIRS], F32, name="dirs")
+        nc.vector.tensor_sub(dirs[:, :, 0:FOLD], ends[:, 1], ends[:, 0])
+        nc.vector.tensor_sub(dirs[:, :, FOLD], x[:, 0:COORDS], x[:, (POINTS - 1) * COORDS : POINTS * COORDS])
+        squares = held.tile([PREDS, COORDS, N_DIRS], F32, name="squares")
+        nc.vector.tensor_mul(squares[:], dirs[:], dirs[:])
+        norm2 = held.tile([PREDS, N_DIRS], F32, name="norm2")
+        nc.vector.tensor_add(norm2[:], squares[:, 0, :], squares[:, 1, :])
+        norm = held.tile([PREDS, N_DIRS], F32, name="norm")
+        nc.gpsimd.tensor_tensor(norm[:], norm2[:], root[:], ALU.pow)
+        norm_eps = held.tile([PREDS, N_DIRS], F32, name="norm_eps")
+        nc.vector.tensor_scalar_add(norm_eps[:], norm[:], EPS)
+        inv_norm = held.tile([PREDS, N_DIRS], F32, name="inv_norm")
+        nc.vector.reciprocal(inv_norm[:], norm_eps[:])
+        unit = held.tile([PREDS, COORDS, N_DIRS], F32, name="unit")
+        nc.vector.tensor_mul(unit[:], dirs[:], inv_norm[:].unsqueeze(1).to_broadcast([PREDS, COORDS, N_DIRS]))
+        un_ps = psum.tile([COORDS, PREDS], F32, name="un_ps")
+        nc.tensor.transpose(un_ps[:], unit[:, :, FOLD], ident[:])
+        vn_ps = psum.tile([COORDS, FOLD, PREDS], F32, name="vn_ps")
+        for i in range(FOLD):
+            nc.tensor.transpose(vn_ps[:, i, :], unit[:, :, i], ident[:])
+        neg_un = held.tile([COORDS, PREDS], F32, name="neg_un")
+        nc.vector.tensor_copy(neg_un[:], un_ps[:])
+        vn = held.tile([COORDS, FOLD, PREDS], F32, name="vn")
+        nc.vector.tensor_copy(vn[:], vn_ps[:])
 
         top = held.tile([PREDS, 1], F32, name="top")
         nc.vector.reduce_max(top[:], logit[:], axis=FREE)
@@ -62,73 +99,40 @@ def tile_hungarianmatcher_kernel(tc, logits, pred_poly, tgt_poly, offs, out):
         neg_prob = held.tile([PREDS, CLASSES], F32, name="neg_prob")
         nc.vector.tensor_scalar(neg_prob[:], expd[:], inv_total[:], -1.0, ALU.mult, ALU.mult)
 
-        last_minus_first = held.tile([POINTS * COORDS, COORDS], F32, name="last_minus_first")
-        nc.vector.tensor_sub(
-            last_minus_first[:],
-            ident[0 : POINTS * COORDS, (POINTS - 1) * COORDS : POINTS * COORDS],
-            ident[0 : POINTS * COORDS, 0:COORDS],
-        )
-        v_ps = psum.tile([BLOCK, N_BLOCKS, COORDS], F32, name="v_ps")
-        for b in range(N_BLOCKS):
-            nc.tensor.matmul(
-                v_ps[:, b, :], y_rows[:, b * BLOCK : (b + 1) * BLOCK], last_minus_first[:], start=True, stop=True
-            )
-        dirs = held.tile([PREDS, 1 + N_BLOCKS, COORDS], F32, name="dirs")
-        nc.vector.tensor_sub(dirs[:, 0, :], x[:, (POINTS - 1) * COORDS : POINTS * COORDS], x[:, 0:COORDS])
-        nc.vector.tensor_copy(dirs[:, 1 : 1 + N_BLOCKS, :], v_ps[:])
-        squares = held.tile([PREDS, 1 + N_BLOCKS, COORDS], F32, name="squares")
-        nc.vector.tensor_mul(squares[:], dirs[:], dirs[:])
-        norm2 = held.tile([PREDS, 1 + N_BLOCKS], F32, name="norm2")
-        nc.vector.reduce_sum(norm2[:], squares[:], axis=FREE)
-        norm = held.tile([PREDS, 1 + N_BLOCKS], F32, name="norm")
-        nc.gpsimd.tensor_tensor(norm[:], norm2[:], halves[:], ALU.pow)
-        norm_eps = held.tile([PREDS, 1 + N_BLOCKS], F32, name="norm_eps")
-        nc.vector.tensor_scalar_add(norm_eps[:], norm[:], EPS)
-        inv_norm = held.tile([PREDS, 1 + N_BLOCKS], F32, name="inv_norm")
-        nc.vector.reciprocal(inv_norm[:], norm_eps[:])
-        unit = held.tile([PREDS, 1 + N_BLOCKS, COORDS], F32, name="unit")
-        nc.vector.tensor_mul(
-            unit[:], dirs[:], inv_norm[:].unsqueeze(2).to_broadcast([PREDS, 1 + N_BLOCKS, COORDS])
-        )
-        un_ps = psum.tile([COORDS, PREDS], F32, name="un_ps")
-        nc.tensor.transpose(un_ps[:], unit[:, 0, :], ident[:])
-        vn_ps = psum.tile([COORDS, TARGETS], F32, name="vn_ps")
-        for b in range(N_BLOCKS):
-            nc.tensor.transpose(vn_ps[:, b * BLOCK : (b + 1) * BLOCK], unit[:, 1 + b, :], ident[:])
-        neg_un = held.tile([COORDS, PREDS], F32, name="neg_un")
-        nc.vector.tensor_scalar_mul(neg_un[:], un_ps[:], -1.0)
-        vn = held.tile([COORDS, TARGETS], F32, name="vn")
-        nc.vector.tensor_copy(vn[:], vn_ps[:])
+        for piece in range(N_PIECES):
+            gaps = gap_pool.tile([PREDS, POINTS, COORDS, POINTS, PIECE], BF16, name="gaps")
+            dist = dist_pool.tile([PREDS, POINTS, POINTS, PIECE], BF16, name="dist")
+            for first_p in range(0, POINTS, HALF):
+                some = slice(first_p, first_p + HALF)
+                for p in range(first_p, first_p + HALF):
+                    for a in range(COORDS):
+                        k = COORDS * p + a
+                        nc.scalar.activation(
+                            gaps[:, p, a], y_all[:, piece, a], FUNC.Abs, bias=x[:, k : k + 1], scale=-1.0
+                        )
+                nc.vector.tensor_tensor(dist[:, some], gaps[:, some, 0], gaps[:, some, 1], ALU.add)
+            two_preds = dist_pool.tile([PREDS, HALF, POINTS, PIECE], BF16, name="two_preds")
+            nc.vector.tensor_tensor(two_preds[:], dist[:, 0:HALF], dist[:, HALF:POINTS], ALU.min)
+            two_tgts = dist_pool.tile([PREDS, POINTS, HALF, PIECE], BF16, name="two_tgts")
+            nc.vector.tensor_tensor(two_tgts[:], dist[:, :, 0:HALF], dist[:, :, HALF:POINTS], ALU.min)
+            near_pred = min_pool.tile([PREDS, POINTS, PIECE], BF16, name="near_pred")
+            nc.vector.tensor_tensor(near_pred[:], two_preds[:, 0], two_preds[:, 1], ALU.min)
+            near_tgt = min_pool.tile([PREDS, POINTS, PIECE], BF16, name="near_tgt")
+            nc.vector.tensor_tensor(near_tgt[:], two_tgts[:, :, 0], two_tgts[:, :, 1], ALU.min)
 
-        for piece in range(TARGETS // PIECE):
-            cols = slice(piece * PIECE, (piece + 1) * PIECE)
             acc = sums.tile([PREDS, PIECE], F32, name="acc")
-            near_pred = work.tile([PREDS, POINTS, PIECE], F32, name="near_pred")
-            for p in range(POINTS):
-                gaps = work.tile([PREDS, COORDS, POINTS, PIECE], F32, name="gaps")
-                for a in range(COORDS):
-                    k = COORDS * p + a
-                    nc.scalar.activation(
-                        gaps[:, a], y_all[:, a, :, cols], FUNC.Abs, bias=x[:, k : k + 1], scale=-1.0
-                    )
-                if p == 0:
-                    dist = near_pred
-                else:
-                    dist = work.tile([PREDS, POINTS, PIECE], F32, name="dist")
-                nc.vector.tensor_tensor(dist[:], gaps[:, 0], gaps[:, 1], ALU.add)
-                pair = work.tile([PREDS, 2, PIECE], F32, name="pair")
-                nc.vector.tensor_tensor(pair[:], dist[:, 0:2], dist[:, 2:4], ALU.min)
-                near_tgt = work.tile([PREDS, PIECE], F32, name="near_tgt")
-                nc.vector.tensor_tensor(near_tgt[:], pair[:, 0], pair[:, 1], ALU.min)
-                nc.tensor.matmul(acc[:], eighth[:], near_tgt[:], start=(p == 0), stop=False)
-                if p > 0:
-                    nc.vector.tensor_tensor(near_pred[:], near_pred[:], dist[:], ALU.min)
-            nc.tensor.matmul(acc[:], neg_un[:], vn[:, cols], start=False, stop=False)
             for q in range(POINTS):
-                nc.tensor.matmul(acc[:], eighth[:], near_pred[:, q], start=False, stop=(q == POINTS - 1))
-            rest = work.tile([PREDS, PIECE], F32, name="rest")
+                nc.tensor.matmul(acc[:], eighth[:], near_pred[:, q], start=(q == 0), stop=False)
+            acc_folded = acc[:].rearrange("c (m i) -> c i m", i=FOLD)
+            folded = slice(piece * (PIECE // FOLD), (piece + 1) * (PIECE // FOLD))
+            for i in range(FOLD):
+                nc.tensor.matmul(acc_folded[:, i, :], neg_un[:], vn[:, i, folded], start=False, stop=False)
+            for p in range(POINTS):
+                nc.tensor.matmul(acc[:], eighth[:], near_tgt[:, p], start=False, stop=(p == POINTS - 1))
+
+            rest = out_pool.tile([PREDS, PIECE], F32, name="rest")
             nc.vector.tensor_scalar_add(rest[:], acc[:], 1.0)
-            cost = work.tile([PREDS, PIECE], F32, name="cost")
+            cost = out_pool.tile([PREDS, PIECE], F32, name="cost")
             picked = neg_prob[:].indirect(offsets[:, piece * (PIECE // 16) : (piece + 1) * (PIECE // 16)])
             nc.vector.tensor_tensor(cost[:], picked, rest[:], ALU.add)
-            nc.sync.dma_start(out[:, cols], cost[:])
+            nc.sync.dma_start(out[:, piece * PIECE : (piece + 1) * PIECE], cost[:])

@@ -12,11 +12,12 @@ PREDS = 128
 CLASSES = 256
 TARGETS = 512
 POINTS = 4
-HALF = POINTS // 2
 COORDS = 2
 EPS = 1e-6
-PIECE = 128
+PIECE = 256
 N_PIECES = TARGETS // PIECE
+SIDES = 2
+SIDE = PIECE // SIDES
 FOLD = TARGETS // PREDS
 N_DIRS = FOLD + 1
 
@@ -27,9 +28,9 @@ def tile_hungarianmatcher_kernel(tc, logits, pred_poly, tgt_poly, offs, out):
     nc = tc.nc
     with (
         tc.tile_pool(name="held", bufs=1) as held,
-        tc.tile_pool(name="gap_pool", bufs=3) as gap_pool,
-        tc.tile_pool(name="dist_pool", bufs=2) as dist_pool,
-        tc.tile_pool(name="min_pool", bufs=N_PIECES) as min_pool,
+        tc.tile_pool(name="gap_pool", bufs=4) as gap_pool,
+        tc.tile_pool(name="dist_pool", bufs=3) as dist_pool,
+        tc.tile_pool(name="min_pool", bufs=2 * POINTS) as min_pool,
         tc.tile_pool(name="out_pool", bufs=2) as out_pool,
         tc.psum_pool(name="psum", bufs=1) as psum,
         tc.psum_pool(name="sums", bufs=N_PIECES) as sums,
@@ -99,36 +100,42 @@ def tile_hungarianmatcher_kernel(tc, logits, pred_poly, tgt_poly, offs, out):
         neg_prob = held.tile([PREDS, CLASSES], F32, name="neg_prob")
         nc.vector.tensor_scalar(neg_prob[:], expd[:], inv_total[:], -1.0, ALU.mult, ALU.mult)
 
+        sides = range(SIDES)
         for piece in range(N_PIECES):
-            gaps = gap_pool.tile([PREDS, POINTS, COORDS, POINTS, PIECE], BF16, name="gaps")
-            dist = dist_pool.tile([PREDS, POINTS, POINTS, PIECE], BF16, name="dist")
-            for first_p in range(0, POINTS, HALF):
-                some = slice(first_p, first_p + HALF)
-                for p in range(first_p, first_p + HALF):
-                    for a in range(COORDS):
-                        k = COORDS * p + a
-                        nc.scalar.activation(
-                            gaps[:, p, a], y_all[:, piece, a], FUNC.Abs, bias=x[:, k : k + 1], scale=-1.0
-                        )
-                nc.vector.tensor_tensor(dist[:, some], gaps[:, some, 0], gaps[:, some, 1], ALU.add)
-            two_preds = dist_pool.tile([PREDS, HALF, POINTS, PIECE], BF16, name="two_preds")
-            nc.vector.tensor_tensor(two_preds[:], dist[:, 0:HALF], dist[:, HALF:POINTS], ALU.min)
-            two_tgts = dist_pool.tile([PREDS, POINTS, HALF, PIECE], BF16, name="two_tgts")
-            nc.vector.tensor_tensor(two_tgts[:], dist[:, :, 0:HALF], dist[:, :, HALF:POINTS], ALU.min)
-            near_pred = min_pool.tile([PREDS, POINTS, PIECE], BF16, name="near_pred")
-            nc.vector.tensor_tensor(near_pred[:], two_preds[:, 0], two_preds[:, 1], ALU.min)
-            near_tgt = min_pool.tile([PREDS, POINTS, PIECE], BF16, name="near_tgt")
-            nc.vector.tensor_tensor(near_tgt[:], two_tgts[:, :, 0], two_tgts[:, :, 1], ALU.min)
-
             acc = sums.tile([PREDS, PIECE], F32, name="acc")
-            for q in range(POINTS):
-                nc.tensor.matmul(acc[:], eighth[:], near_pred[:, q], start=(q == 0), stop=False)
             acc_folded = acc[:].rearrange("c (m i) -> c i m", i=FOLD)
             folded = slice(piece * (PIECE // FOLD), (piece + 1) * (PIECE // FOLD))
             for i in range(FOLD):
-                nc.tensor.matmul(acc_folded[:, i, :], neg_un[:], vn[:, i, folded], start=False, stop=False)
+                nc.tensor.matmul(acc_folded[:, i, :], neg_un[:], vn[:, i, folded], start=(i == 0), stop=False)
+            near_pred = [dist_pool.tile([PREDS, POINTS, SIDE], BF16, name=f"near_pred{s}") for s in sides]
             for p in range(POINTS):
-                nc.tensor.matmul(acc[:], eighth[:], near_tgt[:, p], start=False, stop=(p == POINTS - 1))
+                gaps = gap_pool.tile([PREDS, COORDS, POINTS, PIECE], BF16, name="gaps")
+                for a in range(COORDS):
+                    k = COORDS * p + a
+                    nc.scalar.activation(gaps[:, a], y_all[:, piece, a], FUNC.Abs, bias=x[:, k : k + 1], scale=-1.0)
+                if p == 0:
+                    dist = near_pred
+                else:
+                    dist = [dist_pool.tile([PREDS, POINTS, SIDE], BF16, name=f"dist{s}") for s in sides]
+                pair = [dist_pool.tile([PREDS, 2, SIDE], BF16, name=f"pair{s}") for s in sides]
+                near_tgt = min_pool.tile([PREDS, PIECE], BF16, name="near_tgt")
+                for s in sides:
+                    cols = slice(s * SIDE, (s + 1) * SIDE)
+                    nc.vector.tensor_tensor(dist[s][:], gaps[:, 0, :, cols], gaps[:, 1, :, cols], ALU.add)
+                for s in sides:
+                    nc.vector.tensor_tensor(pair[s][:], dist[s][:, 0:2], dist[s][:, 2:4], ALU.min)
+                if p > 0:
+                    for s in sides:
+                        nc.vector.tensor_tensor(near_pred[s][:], near_pred[s][:], dist[s][:], ALU.min)
+                for s in sides:
+                    cols = slice(s * SIDE, (s + 1) * SIDE)
+                    nc.vector.tensor_tensor(near_tgt[:, cols], pair[s][:, 0], pair[s][:, 1], ALU.min)
+                nc.tensor.matmul(acc[:], eighth[:], near_tgt[:], start=False, stop=False)
+            for s in sides:
+                cols = slice(s * SIDE, (s + 1) * SIDE)
+                for q in range(POINTS):
+                    last = s == SIDES - 1 and q == POINTS - 1
+                    nc.tensor.matmul(acc[:, cols], eighth[:], near_pred[s][:, q], start=False, stop=last)
 
             rest = out_pool.tile([PREDS, PIECE], F32, name="rest")
             nc.vector.tensor_scalar_add(rest[:], acc[:], 1.0)

@@ -14,10 +14,8 @@ TARGETS = 512
 POINTS = 4
 COORDS = 2
 EPS = 1e-6
-PIECE = 256
+PIECE = 128
 N_PIECES = TARGETS // PIECE
-SIDES = 2
-SIDE = PIECE // SIDES
 FOLD = TARGETS // PREDS
 N_DIRS = FOLD + 1
 
@@ -33,23 +31,23 @@ def tile_hungarianmatcher_kernel(tc, logits, pred_poly, tgt_poly, offs, out):
         tc.tile_pool(name="min_pool", bufs=2 * POINTS) as min_pool,
         tc.tile_pool(name="out_pool", bufs=2) as out_pool,
         tc.psum_pool(name="psum", bufs=1) as psum,
-        tc.psum_pool(name="sums", bufs=N_PIECES) as sums,
+        tc.psum_pool(name="sums", bufs=2) as sums,
     ):
         x = held.tile([PREDS, POINTS * COORDS], F32, name="x")
         nc.sync.dma_start(x[:], pred_poly)
+        y_all = held.tile([PREDS, COORDS, POINTS, TARGETS], F32, name="y_all")
+        y_by_coord = tgt_poly.rearrange("(q a) j -> a q j", a=COORDS)
         ends = held.tile([PREDS, 2, COORDS, FOLD], F32, name="ends")
         y_folded = tgt_poly.rearrange("(q a) (m i) -> q m a i", a=COORDS, i=FOLD)
-        nc.scalar.dma_start(ends[:, 0], y_folded[0])
-        nc.scalar.dma_start(ends[:, 1], y_folded[POINTS - 1])
-        y_all = held.tile([PREDS, N_PIECES, COORDS, POINTS, PIECE], F32, name="y_all")
-        y_by_coord = tgt_poly.rearrange("(q a) j -> a q j", a=COORDS)
         logit = held.tile([PREDS, CLASSES], F32, name="logit")
         for piece in range(N_PIECES):
             cols = slice(piece * PIECE, (piece + 1) * PIECE)
-            for a, queue in enumerate((nc.sync, nc.scalar)):
+            for a in range(COORDS):
                 source = y_by_coord[a, :, cols].unsqueeze(0).to_broadcast([PREDS, POINTS, PIECE])
-                queue.dma_start(y_all[:, piece, a], source)
+                nc.sync.dma_start(y_all[:, a, :, cols], source)
             if piece == 0:
+                nc.sync.dma_start(ends[:, 0], y_folded[0])
+                nc.sync.dma_start(ends[:, 1], y_folded[POINTS - 1])
                 nc.sync.dma_start(logit[:], logits)
         offsets = held.tile([PREDS, TARGETS // 16], U16, name="offsets")
         nc.sync.dma_start(offsets[:], offs)
@@ -87,6 +85,12 @@ def tile_hungarianmatcher_kernel(tc, logits, pred_poly, tgt_poly, offs, out):
         nc.vector.tensor_copy(neg_un[:], un_ps[:])
         vn = held.tile([COORDS, FOLD, PREDS], F32, name="vn")
         nc.vector.tensor_copy(vn[:], vn_ps[:])
+        neg_cos = psum.tile([PREDS, TARGETS], F32, name="neg_cos")
+        neg_cos_folded = neg_cos[:].rearrange("c (m i) -> c i m", i=FOLD)
+        for i in range(FOLD):
+            nc.tensor.matmul(neg_cos_folded[:, i, :], neg_un[:], vn[:, i, :], start=(i == 0), stop=(i == FOLD - 1))
+        turn = held.tile([PREDS, TARGETS], F32, name="turn")
+        nc.vector.tensor_scalar_add(turn[:], neg_cos[:], 1.0)
 
         top = held.tile([PREDS, 1], F32, name="top")
         nc.vector.reduce_max(top[:], logit[:], axis=FREE)
@@ -100,46 +104,48 @@ def tile_hungarianmatcher_kernel(tc, logits, pred_poly, tgt_poly, offs, out):
         neg_prob = held.tile([PREDS, CLASSES], F32, name="neg_prob")
         nc.vector.tensor_scalar(neg_prob[:], expd[:], inv_total[:], -1.0, ALU.mult, ALU.mult)
 
-        sides = range(SIDES)
-        for piece in range(N_PIECES):
-            acc = sums.tile([PREDS, PIECE], F32, name="acc")
-            acc_folded = acc[:].rearrange("c (m i) -> c i m", i=FOLD)
-            folded = slice(piece * (PIECE // FOLD), (piece + 1) * (PIECE // FOLD))
-            for i in range(FOLD):
-                nc.tensor.matmul(acc_folded[:, i, :], neg_un[:], vn[:, i, folded], start=(i == 0), stop=False)
-            near_pred = [dist_pool.tile([PREDS, POINTS, SIDE], BF16, name=f"near_pred{s}") for s in sides]
-            for p in range(POINTS):
+        two_costs = held.tile([PREDS, TARGETS], F32, name="two_costs")
+        for first in range(0, TARGETS, CLASSES):
+            cols = slice(first, first + CLASSES)
+            picked = neg_prob[:].indirect(offsets[:, first // 16 : (first + CLASSES) // 16])
+            nc.vector.tensor_tensor(two_costs[:, cols], picked, turn[:, cols], ALU.add)
+
+        units = [(piece, p) for piece in range(N_PIECES) for p in range(POINTS)]
+        dist, pair, near_pred, chamfer = {}, {}, {}, {}
+        for u in range(len(units) + 2):
+            if u < len(units):
+                piece, p = units[u]
+                cols = slice(piece * PIECE, (piece + 1) * PIECE)
                 gaps = gap_pool.tile([PREDS, COORDS, POINTS, PIECE], BF16, name="gaps")
                 for a in range(COORDS):
                     k = COORDS * p + a
-                    nc.scalar.activation(gaps[:, a], y_all[:, piece, a], FUNC.Abs, bias=x[:, k : k + 1], scale=-1.0)
+                    nc.scalar.activation(gaps[:, a], y_all[:, a, :, cols], FUNC.Abs, bias=x[:, k : k + 1], scale=-1.0)
                 if p == 0:
-                    dist = near_pred
+                    near_pred[piece] = dist_pool.tile([PREDS, POINTS, PIECE], BF16, name="near_pred")
+                    dist[u] = near_pred[piece]
                 else:
-                    dist = [dist_pool.tile([PREDS, POINTS, SIDE], BF16, name=f"dist{s}") for s in sides]
-                pair = [dist_pool.tile([PREDS, 2, SIDE], BF16, name=f"pair{s}") for s in sides]
-                near_tgt = min_pool.tile([PREDS, PIECE], BF16, name="near_tgt")
-                for s in sides:
-                    cols = slice(s * SIDE, (s + 1) * SIDE)
-                    nc.vector.tensor_tensor(dist[s][:], gaps[:, 0, :, cols], gaps[:, 1, :, cols], ALU.add)
-                for s in sides:
-                    nc.vector.tensor_tensor(pair[s][:], dist[s][:, 0:2], dist[s][:, 2:4], ALU.min)
+                    dist[u] = dist_pool.tile([PREDS, POINTS, PIECE], BF16, name="dist")
+                nc.vector.tensor_tensor(dist[u][:], gaps[:, 0], gaps[:, 1], ALU.add)
+            if 1 <= u <= len(units):
+                piece, p = units[u - 1]
                 if p > 0:
-                    for s in sides:
-                        nc.vector.tensor_tensor(near_pred[s][:], near_pred[s][:], dist[s][:], ALU.min)
-                for s in sides:
-                    cols = slice(s * SIDE, (s + 1) * SIDE)
-                    nc.vector.tensor_tensor(near_tgt[:, cols], pair[s][:, 0], pair[s][:, 1], ALU.min)
-                nc.tensor.matmul(acc[:], eighth[:], near_tgt[:], start=False, stop=False)
-            for s in sides:
-                cols = slice(s * SIDE, (s + 1) * SIDE)
-                for q in range(POINTS):
-                    last = s == SIDES - 1 and q == POINTS - 1
-                    nc.tensor.matmul(acc[:, cols], eighth[:], near_pred[s][:, q], start=False, stop=last)
-
-            rest = out_pool.tile([PREDS, PIECE], F32, name="rest")
-            nc.vector.tensor_scalar_add(rest[:], acc[:], 1.0)
-            cost = out_pool.tile([PREDS, PIECE], F32, name="cost")
-            picked = neg_prob[:].indirect(offsets[:, piece * (PIECE // 16) : (piece + 1) * (PIECE // 16)])
-            nc.vector.tensor_tensor(cost[:], picked, rest[:], ALU.add)
-            nc.sync.dma_start(out[:, piece * PIECE : (piece + 1) * PIECE], cost[:])
+                    nc.vector.tensor_tensor(near_pred[piece][:], near_pred[piece][:], dist[u - 1][:], ALU.min)
+            if u < len(units):
+                pair[u] = dist_pool.tile([PREDS, 2, PIECE], BF16, name="pair")
+                nc.vector.tensor_tensor(pair[u][:], dist[u][:, 0:2], dist[u][:, 2:4], ALU.min)
+            if 1 <= u <= len(units):
+                piece, p = units[u - 1]
+                near_tgt = min_pool.tile([PREDS, PIECE], BF16, name="near_tgt")
+                nc.vector.tensor_tensor(near_tgt[:], pair[u - 1][:, 0], pair[u - 1][:, 1], ALU.min)
+                if p == 0:
+                    chamfer[piece] = sums.tile([PREDS, PIECE], F32, name="chamfer")
+                if p == POINTS - 1:
+                    for q in range(POINTS):
+                        nc.tensor.matmul(chamfer[piece][:], eighth[:], near_pred[piece][:, q], start=False, stop=False)
+                nc.tensor.matmul(chamfer[piece][:], eighth[:], near_tgt[:], start=(p == 0), stop=(p == POINTS - 1))
+            if u >= 2 and units[u - 2][1] == POINTS - 1:
+                piece = units[u - 2][0]
+                cols = slice(piece * PIECE, (piece + 1) * PIECE)
+                cost = out_pool.tile([PREDS, PIECE], F32, name="cost")
+                nc.vector.tensor_tensor(cost[:], chamfer[piece][:], two_costs[:, cols], ALU.add)
+                nc.sync.dma_start(out[:, cols], cost[:])

@@ -16,6 +16,8 @@ COORDS = 2
 EPS = 1e-6
 PIECE = 128
 N_PIECES = TARGETS // PIECE
+DUO = 2
+VECTOR_S_SHARE = POINTS * COORDS - 1
 FOLD = TARGETS // PREDS
 N_DIRS = FOLD + 1
 
@@ -26,40 +28,39 @@ def tile_hungarianmatcher_kernel(tc, logits, pred_poly, tgt_poly, offs, out):
     nc = tc.nc
     with (
         tc.tile_pool(name="held", bufs=1) as held,
-        tc.tile_pool(name="gap_pool", bufs=4) as gap_pool,
+        tc.tile_pool(name="gap_pool", bufs=3) as gap_pool,
+        tc.tile_pool(name="diff_pool", bufs=2) as diff_pool,
         tc.tile_pool(name="dist_pool", bufs=3) as dist_pool,
-        tc.tile_pool(name="min_pool", bufs=2 * POINTS) as min_pool,
         tc.tile_pool(name="out_pool", bufs=2) as out_pool,
         tc.psum_pool(name="psum", bufs=1) as psum,
-        tc.psum_pool(name="sums", bufs=2) as sums,
     ):
         x = held.tile([PREDS, POINTS * COORDS], F32, name="x")
-        nc.sync.dma_start(x[:], pred_poly)
-        y_all = held.tile([PREDS, COORDS, POINTS, TARGETS], F32, name="y_all")
-        y_by_coord = tgt_poly.rearrange("(q a) j -> a q j", a=COORDS)
         ends = held.tile([PREDS, 2, COORDS, FOLD], F32, name="ends")
         y_folded = tgt_poly.rearrange("(q a) (m i) -> q m a i", a=COORDS, i=FOLD)
+        y_all = held.tile([PREDS, COORDS, POINTS, TARGETS], F32, name="y_all")
+        y_by_coord = tgt_poly.rearrange("(q a) j -> a q j", a=COORDS)
         logit = held.tile([PREDS, CLASSES], F32, name="logit")
+        offsets = held.tile([PREDS, TARGETS // 16], U16, name="offsets")
+        nc.sync.dma_start(x[:], pred_poly)
+        nc.sync.dma_start(ends[:, 0], y_folded[0])
+        nc.sync.dma_start(ends[:, 1], y_folded[POINTS - 1])
         for piece in range(N_PIECES):
             cols = slice(piece * PIECE, (piece + 1) * PIECE)
             for a in range(COORDS):
                 source = y_by_coord[a, :, cols].unsqueeze(0).to_broadcast([PREDS, POINTS, PIECE])
                 nc.sync.dma_start(y_all[:, a, :, cols], source)
             if piece == 0:
-                nc.sync.dma_start(ends[:, 0], y_folded[0])
-                nc.sync.dma_start(ends[:, 1], y_folded[POINTS - 1])
                 nc.sync.dma_start(logit[:], logits)
-        offsets = held.tile([PREDS, TARGETS // 16], U16, name="offsets")
-        nc.sync.dma_start(offsets[:], offs)
+                nc.sync.dma_start(offsets[:], offs)
 
-        ident = held.tile([PREDS, PREDS], F32, name="ident")
-        make_identity(nc, ident[:])
         root = held.tile([PREDS, N_DIRS], F32, name="root")
         nc.gpsimd.memset(root[:], 0.5)
-        eighth = held.tile([PREDS, PREDS], BF16, name="eighth")
-        nc.vector.tensor_scalar_mul(eighth[:], ident[:], 1.0 / (2 * POINTS))
         warm = held.tile([PREDS, N_DIRS], F32, name="warm")
         nc.scalar.activation(warm[:], root[:], FUNC.Exp)
+        ident = held.tile([PREDS, PREDS], F32, name="ident")
+        make_identity(nc, ident[:])
+        eighth = held.tile([PREDS, PREDS], BF16, name="eighth")
+        nc.gpsimd.tensor_scalar_mul(eighth[:], ident[:], 1.0 / (2 * POINTS))
 
         dirs = held.tile([PREDS, COORDS, N_DIRS], F32, name="dirs")
         nc.vector.tensor_sub(dirs[:, :, 0:FOLD], ends[:, 1], ends[:, 0])
@@ -70,82 +71,97 @@ def tile_hungarianmatcher_kernel(tc, logits, pred_poly, tgt_poly, offs, out):
         nc.vector.tensor_add(norm2[:], squares[:, 0, :], squares[:, 1, :])
         norm = held.tile([PREDS, N_DIRS], F32, name="norm")
         nc.gpsimd.tensor_tensor(norm[:], norm2[:], root[:], ALU.pow)
-        norm_eps = held.tile([PREDS, N_DIRS], F32, name="norm_eps")
-        nc.vector.tensor_scalar_add(norm_eps[:], norm[:], EPS)
-        inv_norm = held.tile([PREDS, N_DIRS], F32, name="inv_norm")
-        nc.vector.reciprocal(inv_norm[:], norm_eps[:])
-        unit = held.tile([PREDS, COORDS, N_DIRS], F32, name="unit")
-        nc.vector.tensor_mul(unit[:], dirs[:], inv_norm[:].unsqueeze(1).to_broadcast([PREDS, COORDS, N_DIRS]))
-        un_ps = psum.tile([COORDS, PREDS], F32, name="un_ps")
-        nc.tensor.transpose(un_ps[:], unit[:, :, FOLD], ident[:])
-        vn_ps = psum.tile([COORDS, FOLD, PREDS], F32, name="vn_ps")
-        for i in range(FOLD):
-            nc.tensor.transpose(vn_ps[:, i, :], unit[:, :, i], ident[:])
-        neg_un = held.tile([COORDS, PREDS], F32, name="neg_un")
-        nc.vector.tensor_copy(neg_un[:], un_ps[:])
-        vn = held.tile([COORDS, FOLD, PREDS], F32, name="vn")
-        nc.vector.tensor_copy(vn[:], vn_ps[:])
-        neg_cos = psum.tile([PREDS, TARGETS], F32, name="neg_cos")
-        neg_cos_folded = neg_cos[:].rearrange("c (m i) -> c i m", i=FOLD)
-        for i in range(FOLD):
-            nc.tensor.matmul(neg_cos_folded[:, i, :], neg_un[:], vn[:, i, :], start=(i == 0), stop=(i == FOLD - 1))
-        turn = held.tile([PREDS, TARGETS], F32, name="turn")
-        nc.vector.tensor_scalar_add(turn[:], neg_cos[:], 1.0)
-
         top = held.tile([PREDS, 1], F32, name="top")
         nc.vector.reduce_max(top[:], logit[:], axis=FREE)
         neg_top = held.tile([PREDS, 1], F32, name="neg_top")
         nc.vector.tensor_scalar_mul(neg_top[:], top[:], -1.0)
+
+        un_ps = psum.tile([COORDS, PREDS], F32, name="un_ps")
+        vn_ps = psum.tile([COORDS, FOLD, PREDS], F32, name="vn_ps")
+        neg_cos = psum.tile([PREDS, TARGETS], F32, name="neg_cos")
+        turn = held.tile([PREDS, TARGETS], F32, name="turn")
         expd = held.tile([PREDS, CLASSES], F32, name="expd")
         total = held.tile([PREDS, 1], F32, name="total")
-        nc.scalar.activation(expd[:], logit[:], FUNC.Exp, bias=neg_top[:], scale=1.0, accum_out=total[:])
-        inv_total = held.tile([PREDS, 1], F32, name="inv_total")
-        nc.vector.reciprocal(inv_total[:], total[:])
         neg_prob = held.tile([PREDS, CLASSES], F32, name="neg_prob")
-        nc.vector.tensor_scalar(neg_prob[:], expd[:], inv_total[:], -1.0, ALU.mult, ALU.mult)
-
         two_costs = held.tile([PREDS, TARGETS], F32, name="two_costs")
-        for first in range(0, TARGETS, CLASSES):
-            cols = slice(first, first + CLASSES)
-            picked = neg_prob[:].indirect(offsets[:, first // 16 : (first + CLASSES) // 16])
-            nc.vector.tensor_tensor(two_costs[:, cols], picked, turn[:, cols], ALU.add)
 
-        units = [(piece, p) for piece in range(N_PIECES) for p in range(POINTS)]
-        dist, pair, near_pred, chamfer = {}, {}, {}, {}
-        for u in range(len(units) + 2):
-            if u < len(units):
-                piece, p = units[u]
-                cols = slice(piece * PIECE, (piece + 1) * PIECE)
-                gaps = gap_pool.tile([PREDS, COORDS, POINTS, PIECE], BF16, name="gaps")
+        def unit_directions():
+            norm_eps = held.tile([PREDS, N_DIRS], F32, name="norm_eps")
+            nc.vector.tensor_scalar_add(norm_eps[:], norm[:], EPS)
+            inv_norm = held.tile([PREDS, N_DIRS], F32, name="inv_norm")
+            nc.vector.reciprocal(inv_norm[:], norm_eps[:])
+            unit = held.tile([PREDS, COORDS, N_DIRS], F32, name="unit")
+            nc.vector.tensor_mul(unit[:], dirs[:], inv_norm[:].unsqueeze(1).to_broadcast([PREDS, COORDS, N_DIRS]))
+            nc.tensor.transpose(un_ps[:], unit[:, :, FOLD], ident[:])
+            for i in range(FOLD):
+                nc.tensor.transpose(vn_ps[:, i, :], unit[:, :, i], ident[:])
+
+        def cosines():
+            neg_un = held.tile([COORDS, PREDS], F32, name="neg_un")
+            nc.vector.tensor_copy(neg_un[:], un_ps[:])
+            vn = held.tile([COORDS, FOLD, PREDS], F32, name="vn")
+            nc.vector.tensor_copy(vn[:], vn_ps[:])
+            neg_cos_folded = neg_cos[:].rearrange("c (m i) -> c i m", i=FOLD)
+            for i in range(FOLD):
+                nc.tensor.matmul(neg_cos_folded[:, i, :], neg_un[:], vn[:, i, :], start=(i == 0), stop=(i == FOLD - 1))
+
+        def exponentials():
+            nc.scalar.activation(expd[:], logit[:], FUNC.Exp, bias=neg_top[:], scale=1.0, accum_out=total[:])
+
+        def direction_cost_and_window():
+            nc.vector.tensor_scalar_add(turn[:], neg_cos[:], 1.0)
+            inv_total = held.tile([PREDS, 1], F32, name="inv_total")
+            nc.vector.reciprocal(inv_total[:], total[:])
+            nc.vector.tensor_scalar(neg_prob[:], expd[:], inv_total[:], -1.0, ALU.mult, ALU.mult)
+
+        def look_up():
+            for first in range(0, TARGETS, CLASSES):
+                picked = neg_prob[:].indirect(offsets[:, first // 16 : (first + CLASSES) // 16])
+                nc.vector.tensor_tensor(two_costs[:, first : first + CLASSES], picked, turn[:, first : first + CLASSES], ALU.add)
+
+        steps = (unit_directions, cosines, exponentials, direction_cost_and_window, look_up)
+
+        chamfer = psum.tile([PREDS, TARGETS], F32, name="chamfer")
+
+        def finish(first, end):
+            cost = out_pool.tile([PREDS, end - first], F32, name="cost")
+            nc.vector.tensor_tensor(cost[:], chamfer[:, first:end], two_costs[:, first:end], ALU.add)
+            nc.sync.dma_start(out[:, first:end], cost[:])
+
+        units = [(piece, duo) for piece in range(N_PIECES) for duo in range(POINTS // DUO)]
+        for u, (piece, duo) in enumerate(units):
+            cols = slice(piece * PIECE, (piece + 1) * PIECE)
+            gaps = gap_pool.tile([PREDS, COORDS, DUO, POINTS, PIECE], BF16, name="gaps")
+            for i in range(DUO):
                 for a in range(COORDS):
-                    k = COORDS * p + a
-                    nc.scalar.activation(gaps[:, a], y_all[:, a, :, cols], FUNC.Abs, bias=x[:, k : k + 1], scale=-1.0)
-                if p == 0:
-                    near_pred[piece] = dist_pool.tile([PREDS, POINTS, PIECE], BF16, name="near_pred")
-                    dist[u] = near_pred[piece]
-                else:
-                    dist[u] = dist_pool.tile([PREDS, POINTS, PIECE], BF16, name="dist")
-                nc.vector.tensor_tensor(dist[u][:], gaps[:, 0], gaps[:, 1], ALU.add)
-            if 1 <= u <= len(units):
-                piece, p = units[u - 1]
-                if p > 0:
-                    nc.vector.tensor_tensor(near_pred[piece][:], near_pred[piece][:], dist[u - 1][:], ALU.min)
-            if u < len(units):
-                pair[u] = dist_pool.tile([PREDS, 2, PIECE], BF16, name="pair")
-                nc.vector.tensor_tensor(pair[u][:], dist[u][:, 0:2], dist[u][:, 2:4], ALU.min)
-            if 1 <= u <= len(units):
-                piece, p = units[u - 1]
-                near_tgt = min_pool.tile([PREDS, PIECE], BF16, name="near_tgt")
-                nc.vector.tensor_tensor(near_tgt[:], pair[u - 1][:, 0], pair[u - 1][:, 1], ALU.min)
-                if p == 0:
-                    chamfer[piece] = sums.tile([PREDS, PIECE], F32, name="chamfer")
-                if p == POINTS - 1:
-                    for q in range(POINTS):
-                        nc.tensor.matmul(chamfer[piece][:], eighth[:], near_pred[piece][:, q], start=False, stop=False)
-                nc.tensor.matmul(chamfer[piece][:], eighth[:], near_tgt[:], start=(p == 0), stop=(p == POINTS - 1))
-            if u >= 2 and units[u - 2][1] == POINTS - 1:
-                piece = units[u - 2][0]
-                cols = slice(piece * PIECE, (piece + 1) * PIECE)
-                cost = out_pool.tile([PREDS, PIECE], F32, name="cost")
-                nc.vector.tensor_tensor(cost[:], chamfer[piece][:], two_costs[:, cols], ALU.add)
-                nc.sync.dma_start(out[:, cols], cost[:])
+                    k = COORDS * (DUO * duo + i) + a
+                    if k == VECTOR_S_SHARE:
+                        above = diff_pool.tile([PREDS, POINTS, PIECE], BF16, name="above")
+                        nc.vector.tensor_scalar_sub(above[:], y_all[:, a, :, cols], x[:, k : k + 1])
+                        below = diff_pool.tile([PREDS, POINTS, PIECE], BF16, name="below")
+                        nc.vector.tensor_scalar(below[:], y_all[:, a, :, cols], -1.0, x[:, k : k + 1], ALU.mult, ALU.add)
+                        nc.vector.tensor_tensor(gaps[:, a, i], above[:], below[:], ALU.max)
+                    else:
+                        nc.scalar.activation(gaps[:, a, i], y_all[:, a, :, cols], FUNC.Abs, bias=x[:, k : k + 1], scale=-1.0)
+            dist = dist_pool.tile([PREDS, DUO, POINTS, PIECE], BF16, name="dist")
+            nc.vector.tensor_tensor(dist[:], gaps[:, 0], gaps[:, 1], ALU.add)
+            lower = dist_pool.tile([PREDS, POINTS, PIECE], BF16, name="lower")
+            nc.vector.tensor_tensor(lower[:], dist[:, 0], dist[:, 1], ALU.min)
+            if duo == 0:
+                lower_before = lower
+            else:
+                near_pred = dist_pool.tile([PREDS, POINTS, PIECE], BF16, name="near_pred")
+                nc.vector.tensor_tensor(near_pred[:], lower_before[:], lower[:], ALU.min)
+                for q in range(POINTS):
+                    nc.tensor.matmul(chamfer[:, cols], eighth[:], near_pred[:, q], start=False, stop=False)
+            pair = dist_pool.tile([PREDS, DUO, 2, PIECE], BF16, name="pair")
+            nc.vector.tensor_tensor(pair[:], dist[:, :, 0:2], dist[:, :, 2:4], ALU.min)
+            near_tgt = dist_pool.tile([PREDS, DUO, PIECE], BF16, name="near_tgt")
+            nc.vector.tensor_tensor(near_tgt[:], pair[:, :, 0], pair[:, :, 1], ALU.min)
+            for i in range(DUO):
+                nc.tensor.matmul(chamfer[:, cols], eighth[:], near_tgt[:, i], start=(duo == 0 and i == 0), stop=(duo == 1 and i == DUO - 1))
+            if u < len(steps):
+                steps[u]()
+            if piece == N_PIECES - 1 and duo == 0:
+                finish(0, piece * PIECE)
+        finish((N_PIECES - 1) * PIECE, TARGETS)

@@ -17,7 +17,8 @@ EPS = 1e-6
 PIECE = 128
 N_PIECES = TARGETS // PIECE
 DUO = 2
-VECTOR_S_SHARE = POINTS * COORDS - 1
+FIRST_SHARE = (2, 3)
+LATER_SHARE = (POINTS * COORDS - 1,)
 FOLD = TARGETS // PREDS
 N_DIRS = FOLD + 1
 
@@ -31,8 +32,8 @@ def tile_hungarianmatcher_kernel(tc, logits, pred_poly, tgt_poly, offs, out):
         tc.tile_pool(name="gap_pool", bufs=3) as gap_pool,
         tc.tile_pool(name="diff_pool", bufs=2) as diff_pool,
         tc.tile_pool(name="dist_pool", bufs=3) as dist_pool,
-        tc.tile_pool(name="out_pool", bufs=2) as out_pool,
         tc.psum_pool(name="psum", bufs=1) as psum,
+        tc.psum_pool(name="sums", bufs=N_PIECES) as sums,
     ):
         x = held.tile([PREDS, POINTS * COORDS], F32, name="x")
         ends = held.tile([PREDS, 2, COORDS, FOLD], F32, name="ends")
@@ -42,8 +43,8 @@ def tile_hungarianmatcher_kernel(tc, logits, pred_poly, tgt_poly, offs, out):
         logit = held.tile([PREDS, CLASSES], F32, name="logit")
         offsets = held.tile([PREDS, TARGETS // 16], U16, name="offsets")
         nc.sync.dma_start(x[:], pred_poly)
-        nc.sync.dma_start(ends[:, 0], y_folded[0])
-        nc.sync.dma_start(ends[:, 1], y_folded[POINTS - 1])
+        nc.scalar.dma_start(ends[:, 0], y_folded[0])
+        nc.scalar.dma_start(ends[:, 1], y_folded[POINTS - 1])
         for piece in range(N_PIECES):
             cols = slice(piece * PIECE, (piece + 1) * PIECE)
             for a in range(COORDS):
@@ -71,10 +72,7 @@ def tile_hungarianmatcher_kernel(tc, logits, pred_poly, tgt_poly, offs, out):
         nc.vector.tensor_add(norm2[:], squares[:, 0, :], squares[:, 1, :])
         norm = held.tile([PREDS, N_DIRS], F32, name="norm")
         nc.gpsimd.tensor_tensor(norm[:], norm2[:], root[:], ALU.pow)
-        top = held.tile([PREDS, 1], F32, name="top")
-        nc.vector.reduce_max(top[:], logit[:], axis=FREE)
         neg_top = held.tile([PREDS, 1], F32, name="neg_top")
-        nc.vector.tensor_scalar_mul(neg_top[:], top[:], -1.0)
 
         un_ps = psum.tile([COORDS, PREDS], F32, name="un_ps")
         vn_ps = psum.tile([COORDS, FOLD, PREDS], F32, name="vn_ps")
@@ -84,8 +82,12 @@ def tile_hungarianmatcher_kernel(tc, logits, pred_poly, tgt_poly, offs, out):
         total = held.tile([PREDS, 1], F32, name="total")
         neg_prob = held.tile([PREDS, CLASSES], F32, name="neg_prob")
         two_costs = held.tile([PREDS, TARGETS], F32, name="two_costs")
+        cost_ps = [sums.tile([PREDS, PIECE], F32, name="cost_ps") for piece in range(N_PIECES)]
 
         def unit_directions():
+            top = held.tile([PREDS, 1], F32, name="top")
+            nc.vector.reduce_max(top[:], logit[:], axis=FREE)
+            nc.vector.tensor_scalar_mul(neg_top[:], top[:], -1.0)
             norm_eps = held.tile([PREDS, N_DIRS], F32, name="norm_eps")
             nc.vector.tensor_scalar_add(norm_eps[:], norm[:], EPS)
             inv_norm = held.tile([PREDS, N_DIRS], F32, name="inv_norm")
@@ -96,46 +98,43 @@ def tile_hungarianmatcher_kernel(tc, logits, pred_poly, tgt_poly, offs, out):
             for i in range(FOLD):
                 nc.tensor.transpose(vn_ps[:, i, :], unit[:, :, i], ident[:])
 
+        def exponentials():
+            nc.scalar.activation(expd[:], logit[:], FUNC.Exp, bias=neg_top[:], scale=1.0, accum_out=total[:])
+
         def cosines():
             neg_un = held.tile([COORDS, PREDS], F32, name="neg_un")
-            nc.vector.tensor_copy(neg_un[:], un_ps[:])
+            nc.scalar.copy(neg_un[:], un_ps[:])
             vn = held.tile([COORDS, FOLD, PREDS], F32, name="vn")
-            nc.vector.tensor_copy(vn[:], vn_ps[:])
+            nc.scalar.copy(vn[:], vn_ps[:])
             neg_cos_folded = neg_cos[:].rearrange("c (m i) -> c i m", i=FOLD)
             for i in range(FOLD):
                 nc.tensor.matmul(neg_cos_folded[:, i, :], neg_un[:], vn[:, i, :], start=(i == 0), stop=(i == FOLD - 1))
 
-        def exponentials():
-            nc.scalar.activation(expd[:], logit[:], FUNC.Exp, bias=neg_top[:], scale=1.0, accum_out=total[:])
-
-        def direction_cost_and_window():
-            nc.vector.tensor_scalar_add(turn[:], neg_cos[:], 1.0)
+        def window():
             inv_total = held.tile([PREDS, 1], F32, name="inv_total")
             nc.vector.reciprocal(inv_total[:], total[:])
             nc.vector.tensor_scalar(neg_prob[:], expd[:], inv_total[:], -1.0, ALU.mult, ALU.mult)
+
+        def direction_cost():
+            nc.scalar.add(turn[:], neg_cos[:], 1.0)
 
         def look_up():
             for first in range(0, TARGETS, CLASSES):
                 picked = neg_prob[:].indirect(offsets[:, first // 16 : (first + CLASSES) // 16])
                 nc.vector.tensor_tensor(two_costs[:, first : first + CLASSES], picked, turn[:, first : first + CLASSES], ALU.add)
-
-        steps = (unit_directions, cosines, exponentials, direction_cost_and_window, look_up)
-
-        chamfer = psum.tile([PREDS, TARGETS], F32, name="chamfer")
-
-        def finish(first, end):
-            cost = out_pool.tile([PREDS, end - first], F32, name="cost")
-            nc.vector.tensor_tensor(cost[:], chamfer[:, first:end], two_costs[:, first:end], ALU.add)
-            nc.sync.dma_start(out[:, first:end], cost[:])
+            for piece in range(N_PIECES):
+                cols = slice(piece * PIECE, (piece + 1) * PIECE)
+                nc.tensor.matmul(cost_ps[piece][:], ident[:], two_costs[:, cols], start=False, stop=(piece < N_PIECES - 1))
 
         units = [(piece, duo) for piece in range(N_PIECES) for duo in range(POINTS // DUO)]
         for u, (piece, duo) in enumerate(units):
             cols = slice(piece * PIECE, (piece + 1) * PIECE)
+            last_piece = piece == N_PIECES - 1
             gaps = gap_pool.tile([PREDS, COORDS, DUO, POINTS, PIECE], BF16, name="gaps")
             for i in range(DUO):
                 for a in range(COORDS):
                     k = COORDS * (DUO * duo + i) + a
-                    if k == VECTOR_S_SHARE:
+                    if k in (FIRST_SHARE if piece == 0 else LATER_SHARE):
                         above = diff_pool.tile([PREDS, POINTS, PIECE], BF16, name="above")
                         nc.vector.tensor_scalar_sub(above[:], y_all[:, a, :, cols], x[:, k : k + 1])
                         below = diff_pool.tile([PREDS, POINTS, PIECE], BF16, name="below")
@@ -153,15 +152,28 @@ def tile_hungarianmatcher_kernel(tc, logits, pred_poly, tgt_poly, offs, out):
                 near_pred = dist_pool.tile([PREDS, POINTS, PIECE], BF16, name="near_pred")
                 nc.vector.tensor_tensor(near_pred[:], lower_before[:], lower[:], ALU.min)
                 for q in range(POINTS):
-                    nc.tensor.matmul(chamfer[:, cols], eighth[:], near_pred[:, q], start=False, stop=False)
+                    nc.tensor.matmul(cost_ps[piece][:], eighth[:], near_pred[:, q], start=False, stop=False)
             pair = dist_pool.tile([PREDS, DUO, 2, PIECE], BF16, name="pair")
             nc.vector.tensor_tensor(pair[:], dist[:, :, 0:2], dist[:, :, 2:4], ALU.min)
             near_tgt = dist_pool.tile([PREDS, DUO, PIECE], BF16, name="near_tgt")
             nc.vector.tensor_tensor(near_tgt[:], pair[:, :, 0], pair[:, :, 1], ALU.min)
             for i in range(DUO):
-                nc.tensor.matmul(chamfer[:, cols], eighth[:], near_tgt[:, i], start=(duo == 0 and i == 0), stop=(duo == 1 and i == DUO - 1))
-            if u < len(steps):
-                steps[u]()
-            if piece == N_PIECES - 1 and duo == 0:
-                finish(0, piece * PIECE)
-        finish((N_PIECES - 1) * PIECE, TARGETS)
+                nc.tensor.matmul(cost_ps[piece][:], eighth[:], near_tgt[:, i], start=(duo == 0 and i == 0), stop=(last_piece and duo == 1 and i == DUO - 1))
+            if u == 0:
+                unit_directions()
+            if u == 2:
+                exponentials()
+            if u == 3:
+                cosines()
+                window()
+            if u == 5:
+                direction_cost()
+            if u == 6:
+                look_up()
+
+        cost = held.tile([PREDS, TARGETS], F32, name="cost")
+        for piece in range(N_PIECES):
+            nc.scalar.copy(cost[:, piece * PIECE : (piece + 1) * PIECE], cost_ps[piece][:])
+            if piece == N_PIECES - 2:
+                nc.sync.dma_start(out[:, 0 : (piece + 1) * PIECE], cost[:, 0 : (piece + 1) * PIECE])
+        nc.sync.dma_start(out[:, (N_PIECES - 1) * PIECE : TARGETS], cost[:, (N_PIECES - 1) * PIECE : TARGETS])

@@ -135,11 +135,9 @@ def tile_hungarianmatcher_kernel(tc, logits, pred_poly, tgt_poly, offs, out):
                 for a in range(COORDS):
                     k = COORDS * (DUO * duo + i) + a
                     if k in (FIRST_SHARE if piece == 0 else LATER_SHARE):
-                        above = diff_pool.tile([PREDS, POINTS, PIECE], BF16, name="above")
-                        nc.vector.tensor_scalar_sub(above[:], y_all[:, a, :, cols], x[:, k : k + 1])
                         below = diff_pool.tile([PREDS, POINTS, PIECE], BF16, name="below")
                         nc.vector.tensor_scalar(below[:], y_all[:, a, :, cols], -1.0, x[:, k : k + 1], ALU.mult, ALU.add)
-                        nc.vector.tensor_tensor(gaps[:, a, i], above[:], below[:], ALU.max)
+                        nc.vector.scalar_tensor_tensor(gaps[:, a, i], y_all[:, a, :, cols], x[:, k : k + 1], below[:], ALU.subtract, ALU.max)
                     else:
                         nc.scalar.activation(gaps[:, a, i], y_all[:, a, :, cols], FUNC.Abs, bias=x[:, k : k + 1], scale=-1.0)
             dist = dist_pool.tile([PREDS, DUO, POINTS, PIECE], BF16, name="dist")

@@ -14,8 +14,9 @@ TARGETS = 512
 POINTS = 4
 COORDS = 2
 EPS = 1e-6
-PIECE = 128
-N_PIECES = TARGETS // PIECE
+PIECE_WIDTHS = (128, 128, 128, 64, 64)
+N_PIECES = len(PIECE_WIDTHS)
+LOOK_UP_IN = 3
 DUO = 2
 FIRST_SHARE = (2, 3)
 LATER_SHARE = (POINTS * COORDS - 1,)
@@ -27,6 +28,8 @@ FLOPS = PREDS * TARGETS * 118
 
 def tile_hungarianmatcher_kernel(tc, logits, pred_poly, tgt_poly, offs, out):
     nc = tc.nc
+    starts = [sum(PIECE_WIDTHS[:piece]) for piece in range(N_PIECES)]
+    columns = [slice(start, start + width) for start, width in zip(starts, PIECE_WIDTHS)]
     with (
         tc.tile_pool(name="held", bufs=1) as held,
         tc.tile_pool(name="gap_pool", bufs=3) as gap_pool,
@@ -45,10 +48,9 @@ def tile_hungarianmatcher_kernel(tc, logits, pred_poly, tgt_poly, offs, out):
         nc.sync.dma_start(x[:], pred_poly)
         nc.scalar.dma_start(ends[:, 0], y_folded[0])
         nc.scalar.dma_start(ends[:, 1], y_folded[POINTS - 1])
-        for piece in range(N_PIECES):
-            cols = slice(piece * PIECE, (piece + 1) * PIECE)
+        for piece, cols in enumerate(columns):
             for a in range(COORDS):
-                source = y_by_coord[a, :, cols].unsqueeze(0).to_broadcast([PREDS, POINTS, PIECE])
+                source = y_by_coord[a, :, cols].unsqueeze(0).to_broadcast([PREDS, POINTS, PIECE_WIDTHS[piece]])
                 nc.sync.dma_start(y_all[:, a, :, cols], source)
             if piece == 0:
                 nc.sync.dma_start(logit[:], logits)
@@ -82,7 +84,7 @@ def tile_hungarianmatcher_kernel(tc, logits, pred_poly, tgt_poly, offs, out):
         total = held.tile([PREDS, 1], F32, name="total")
         neg_prob = held.tile([PREDS, CLASSES], F32, name="neg_prob")
         two_costs = held.tile([PREDS, TARGETS], F32, name="two_costs")
-        cost_ps = [sums.tile([PREDS, PIECE], F32, name="cost_ps") for piece in range(N_PIECES)]
+        cost_ps = [sums.tile([PREDS, width], F32, name="cost_ps") for width in PIECE_WIDTHS]
 
         def unit_directions():
             top = held.tile([PREDS, 1], F32, name="top")
@@ -122,41 +124,39 @@ def tile_hungarianmatcher_kernel(tc, logits, pred_poly, tgt_poly, offs, out):
             for first in range(0, TARGETS, CLASSES):
                 picked = neg_prob[:].indirect(offsets[:, first // 16 : (first + CLASSES) // 16])
                 nc.vector.tensor_tensor(two_costs[:, first : first + CLASSES], picked, turn[:, first : first + CLASSES], ALU.add)
-            for piece in range(N_PIECES):
-                cols = slice(piece * PIECE, (piece + 1) * PIECE)
-                nc.tensor.matmul(cost_ps[piece][:], ident[:], two_costs[:, cols], start=False, stop=(piece < N_PIECES - 1))
+            for piece, cols in enumerate(columns):
+                nc.tensor.matmul(cost_ps[piece][:], ident[:], two_costs[:, cols], start=(piece > LOOK_UP_IN), stop=(piece < LOOK_UP_IN))
 
         units = [(piece, duo) for piece in range(N_PIECES) for duo in range(POINTS // DUO)]
         for u, (piece, duo) in enumerate(units):
-            cols = slice(piece * PIECE, (piece + 1) * PIECE)
-            last_piece = piece == N_PIECES - 1
-            gaps = gap_pool.tile([PREDS, COORDS, DUO, POINTS, PIECE], BF16, name="gaps")
+            cols, width = columns[piece], PIECE_WIDTHS[piece]
+            gaps = gap_pool.tile([PREDS, COORDS, DUO, POINTS, width], BF16, name="gaps")
             for i in range(DUO):
                 for a in range(COORDS):
                     k = COORDS * (DUO * duo + i) + a
                     if k in (FIRST_SHARE if piece == 0 else LATER_SHARE):
-                        below = diff_pool.tile([PREDS, POINTS, PIECE], BF16, name="below")
+                        below = diff_pool.tile([PREDS, POINTS, width], BF16, name="below")
                         nc.vector.tensor_scalar(below[:], y_all[:, a, :, cols], -1.0, x[:, k : k + 1], ALU.mult, ALU.add)
                         nc.vector.scalar_tensor_tensor(gaps[:, a, i], y_all[:, a, :, cols], x[:, k : k + 1], below[:], ALU.subtract, ALU.max)
                     else:
                         nc.scalar.activation(gaps[:, a, i], y_all[:, a, :, cols], FUNC.Abs, bias=x[:, k : k + 1], scale=-1.0)
-            dist = dist_pool.tile([PREDS, DUO, POINTS, PIECE], BF16, name="dist")
+            dist = dist_pool.tile([PREDS, DUO, POINTS, width], BF16, name="dist")
             nc.vector.tensor_tensor(dist[:], gaps[:, 0], gaps[:, 1], ALU.add)
-            lower = dist_pool.tile([PREDS, POINTS, PIECE], BF16, name="lower")
+            lower = dist_pool.tile([PREDS, POINTS, width], BF16, name="lower")
             nc.vector.tensor_tensor(lower[:], dist[:, 0], dist[:, 1], ALU.min)
             if duo == 0:
                 lower_before = lower
             else:
-                near_pred = dist_pool.tile([PREDS, POINTS, PIECE], BF16, name="near_pred")
+                near_pred = dist_pool.tile([PREDS, POINTS, width], BF16, name="near_pred")
                 nc.vector.tensor_tensor(near_pred[:], lower_before[:], lower[:], ALU.min)
                 for q in range(POINTS):
                     nc.tensor.matmul(cost_ps[piece][:], eighth[:], near_pred[:, q], start=False, stop=False)
-            pair = dist_pool.tile([PREDS, DUO, 2, PIECE], BF16, name="pair")
+            pair = dist_pool.tile([PREDS, DUO, 2, width], BF16, name="pair")
             nc.vector.tensor_tensor(pair[:], dist[:, :, 0:2], dist[:, :, 2:4], ALU.min)
-            near_tgt = dist_pool.tile([PREDS, DUO, PIECE], BF16, name="near_tgt")
+            near_tgt = dist_pool.tile([PREDS, DUO, width], BF16, name="near_tgt")
             nc.vector.tensor_tensor(near_tgt[:], pair[:, :, 0], pair[:, :, 1], ALU.min)
             for i in range(DUO):
-                nc.tensor.matmul(cost_ps[piece][:], eighth[:], near_tgt[:, i], start=(duo == 0 and i == 0), stop=(last_piece and duo == 1 and i == DUO - 1))
+                nc.tensor.matmul(cost_ps[piece][:], eighth[:], near_tgt[:, i], start=(piece <= LOOK_UP_IN and duo == 0 and i == 0), stop=(piece >= LOOK_UP_IN and duo == 1 and i == DUO - 1))
             if u == 0:
                 unit_directions()
             if u == 2:
@@ -166,12 +166,12 @@ def tile_hungarianmatcher_kernel(tc, logits, pred_poly, tgt_poly, offs, out):
                 window()
             if u == 5:
                 direction_cost()
-            if u == 6:
+            if piece == LOOK_UP_IN and duo == 0:
                 look_up()
 
         cost = held.tile([PREDS, TARGETS], F32, name="cost")
-        for piece in range(N_PIECES):
-            nc.scalar.copy(cost[:, piece * PIECE : (piece + 1) * PIECE], cost_ps[piece][:])
+        for piece, cols in enumerate(columns):
+            nc.scalar.copy(cost[:, cols], cost_ps[piece][:])
             if piece == N_PIECES - 2:
-                nc.sync.dma_start(out[:, 0 : (piece + 1) * PIECE], cost[:, 0 : (piece + 1) * PIECE])
-        nc.sync.dma_start(out[:, (N_PIECES - 1) * PIECE : TARGETS], cost[:, (N_PIECES - 1) * PIECE : TARGETS])
+                nc.sync.dma_start(out[:, 0 : cols.stop], cost[:, 0 : cols.stop])
+        nc.sync.dma_start(out[:, columns[-1]], cost[:, columns[-1]])

@@ -16,10 +16,10 @@ COORDS = 2
 EPS = 1e-6
 PIECE_WIDTHS = (128, 128, 128, 64, 64)
 N_PIECES = len(PIECE_WIDTHS)
-LOOK_UP_IN = 3
-DUO = 2
-FIRST_SHARE = (2, 3)
-LATER_SHARE = (POINTS * COORDS - 1,)
+COSINE_FROM = 3
+HALF = POINTS // 2
+FIRST_SHARE = (0, 1)
+LATER_SHARE = (POINTS - 1,)
 FOLD = TARGETS // PREDS
 N_DIRS = FOLD + 1
 
@@ -33,10 +33,10 @@ def tile_hungarianmatcher_kernel(tc, logits, pred_poly, tgt_poly, offs, out):
     with (
         tc.tile_pool(name="held", bufs=1) as held,
         tc.tile_pool(name="gap_pool", bufs=3) as gap_pool,
-        tc.tile_pool(name="diff_pool", bufs=2) as diff_pool,
+        tc.tile_pool(name="lift_pool", bufs=3) as lift_pool,
         tc.tile_pool(name="dist_pool", bufs=3) as dist_pool,
-        tc.psum_pool(name="psum", bufs=1) as psum,
-        tc.psum_pool(name="sums", bufs=N_PIECES) as sums,
+        tc.psum_pool(name="far_pool", bufs=3) as far_pool,
+        tc.psum_pool(name="sums", bufs=4) as sums,
     ):
         x = held.tile([PREDS, POINTS * COORDS], F32, name="x")
         ends = held.tile([PREDS, 2, COORDS, FOLD], F32, name="ends")
@@ -46,132 +46,146 @@ def tile_hungarianmatcher_kernel(tc, logits, pred_poly, tgt_poly, offs, out):
         logit = held.tile([PREDS, CLASSES], F32, name="logit")
         offsets = held.tile([PREDS, TARGETS // 16], U16, name="offsets")
         nc.sync.dma_start(x[:], pred_poly)
-        nc.scalar.dma_start(ends[:, 0], y_folded[0])
-        nc.scalar.dma_start(ends[:, 1], y_folded[POINTS - 1])
         for piece, cols in enumerate(columns):
             for a in range(COORDS):
                 source = y_by_coord[a, :, cols].unsqueeze(0).to_broadcast([PREDS, POINTS, PIECE_WIDTHS[piece]])
                 nc.sync.dma_start(y_all[:, a, :, cols], source)
-            if piece == 0:
+            if piece == 1:
+                nc.sync.dma_start(ends[:, 0], y_folded[0])
+                nc.sync.dma_start(ends[:, 1], y_folded[POINTS - 1])
                 nc.sync.dma_start(logit[:], logits)
                 nc.sync.dma_start(offsets[:], offs)
 
         root = held.tile([PREDS, N_DIRS], F32, name="root")
         nc.gpsimd.memset(root[:], 0.5)
+        minus_one = held.tile([PREDS, N_DIRS], F32, name="minus_one")
+        nc.gpsimd.memset(minus_one[:], -1.0)
         warm = held.tile([PREDS, N_DIRS], F32, name="warm")
         nc.scalar.activation(warm[:], root[:], FUNC.Exp)
+        one = held.tile([PREDS, PREDS], BF16, name="one")
+        make_identity(nc, one[:])
+        eighth = held.tile([PREDS, PREDS], BF16, name="eighth")
+        nc.gpsimd.tensor_scalar_mul(eighth[:], one[:], 1.0 / (2 * POINTS))
         ident = held.tile([PREDS, PREDS], F32, name="ident")
         make_identity(nc, ident[:])
-        eighth = held.tile([PREDS, PREDS], BF16, name="eighth")
-        nc.gpsimd.tensor_scalar_mul(eighth[:], ident[:], 1.0 / (2 * POINTS))
 
-        dirs = held.tile([PREDS, COORDS, N_DIRS], F32, name="dirs")
-        nc.vector.tensor_sub(dirs[:, :, 0:FOLD], ends[:, 1], ends[:, 0])
-        nc.vector.tensor_sub(dirs[:, :, FOLD], x[:, 0:COORDS], x[:, (POINTS - 1) * COORDS : POINTS * COORDS])
-        squares = held.tile([PREDS, COORDS, N_DIRS], F32, name="squares")
-        nc.vector.tensor_mul(squares[:], dirs[:], dirs[:])
-        norm2 = held.tile([PREDS, N_DIRS], F32, name="norm2")
-        nc.vector.tensor_add(norm2[:], squares[:, 0, :], squares[:, 1, :])
-        norm = held.tile([PREDS, N_DIRS], F32, name="norm")
-        nc.gpsimd.tensor_tensor(norm[:], norm2[:], root[:], ALU.pow)
         neg_top = held.tile([PREDS, 1], F32, name="neg_top")
-
-        un_ps = psum.tile([COORDS, PREDS], F32, name="un_ps")
-        vn_ps = psum.tile([COORDS, FOLD, PREDS], F32, name="vn_ps")
-        neg_cos = psum.tile([PREDS, TARGETS], F32, name="neg_cos")
-        turn = held.tile([PREDS, TARGETS], F32, name="turn")
+        neg_un = held.tile([COORDS, PREDS], F32, name="neg_un")
+        vn = held.tile([COORDS, TARGETS], F32, name="vn")
         expd = held.tile([PREDS, CLASSES], F32, name="expd")
         total = held.tile([PREDS, 1], F32, name="total")
         neg_prob = held.tile([PREDS, CLASSES], F32, name="neg_prob")
         two_costs = held.tile([PREDS, TARGETS], F32, name="two_costs")
-        cost_ps = [sums.tile([PREDS, width], F32, name="cost_ps") for width in PIECE_WIDTHS]
+        cost = held.tile([PREDS, TARGETS], F32, name="cost")
+        dirs = held.tile([PREDS, COORDS, N_DIRS], F32, name="dirs")
+        unit = held.tile([PREDS, COORDS, N_DIRS], F32, name="unit")
 
         def unit_directions():
+            nc.gpsimd.tensor_sub(dirs[:, :, 0:FOLD], ends[:, 1], ends[:, 0])
+            nc.gpsimd.tensor_sub(dirs[:, :, FOLD], x[:, 0:COORDS], x[:, (POINTS - 1) * COORDS : POINTS * COORDS])
+            squares = held.tile([PREDS, COORDS, N_DIRS], F32, name="squares")
+            nc.gpsimd.tensor_mul(squares[:], dirs[:], dirs[:])
+            norm2 = held.tile([PREDS, N_DIRS], F32, name="norm2")
+            nc.gpsimd.tensor_add(norm2[:], squares[:, 0, :], squares[:, 1, :])
+            norm = held.tile([PREDS, N_DIRS], F32, name="norm")
+            nc.gpsimd.tensor_tensor(norm[:], norm2[:], root[:], ALU.pow)
+            norm_eps = held.tile([PREDS, N_DIRS], F32, name="norm_eps")
+            nc.gpsimd.tensor_scalar_add(norm_eps[:], norm[:], EPS)
+            inv_norm = held.tile([PREDS, N_DIRS], F32, name="inv_norm")
+            nc.gpsimd.tensor_tensor(inv_norm[:], norm_eps[:], minus_one[:], ALU.pow)
+            for a in range(COORDS):
+                nc.gpsimd.tensor_mul(unit[:, a], dirs[:, a], inv_norm[:])
+
+        def top_logits():
             top = held.tile([PREDS, 1], F32, name="top")
             nc.vector.reduce_max(top[:], logit[:], axis=FREE)
-            nc.vector.tensor_scalar_mul(neg_top[:], top[:], -1.0)
-            norm_eps = held.tile([PREDS, N_DIRS], F32, name="norm_eps")
-            nc.vector.tensor_scalar_add(norm_eps[:], norm[:], EPS)
-            inv_norm = held.tile([PREDS, N_DIRS], F32, name="inv_norm")
-            nc.vector.reciprocal(inv_norm[:], norm_eps[:])
-            unit = held.tile([PREDS, COORDS, N_DIRS], F32, name="unit")
-            nc.vector.tensor_mul(unit[:], dirs[:], inv_norm[:].unsqueeze(1).to_broadcast([PREDS, COORDS, N_DIRS]))
-            nc.tensor.transpose(un_ps[:], unit[:, :, FOLD], ident[:])
+            nc.gpsimd.tensor_scalar_mul(neg_top[:], top[:], -1.0)
+
+        def flipped_directions():
+            vn_ps = far_pool.tile([COORDS, FOLD, PREDS], F32, name="vn_ps", tag="far")
+            un_ps = far_pool.tile([COORDS, PREDS], F32, name="un_ps", tag="far")
             for i in range(FOLD):
                 nc.tensor.transpose(vn_ps[:, i, :], unit[:, :, i], ident[:])
+            nc.tensor.transpose(un_ps[:], unit[:, :, FOLD], ident[:])
+            nc.scalar.copy(neg_un[:], un_ps[:])
+            nc.scalar.copy(vn[:].rearrange("a (m i) -> a m i", i=FOLD), vn_ps[:].rearrange("a i m -> a m i"))
 
         def exponentials():
             nc.scalar.activation(expd[:], logit[:], FUNC.Exp, bias=neg_top[:], scale=1.0, accum_out=total[:])
 
-        def cosines():
-            neg_un = held.tile([COORDS, PREDS], F32, name="neg_un")
-            nc.scalar.copy(neg_un[:], un_ps[:])
-            vn = held.tile([COORDS, FOLD, PREDS], F32, name="vn")
-            nc.scalar.copy(vn[:], vn_ps[:])
-            neg_cos_folded = neg_cos[:].rearrange("c (m i) -> c i m", i=FOLD)
-            for i in range(FOLD):
-                nc.tensor.matmul(neg_cos_folded[:, i, :], neg_un[:], vn[:, i, :], start=(i == 0), stop=(i == FOLD - 1))
+        def cosine(piece):
+            nc.tensor.matmul(cost_ps[piece][:], neg_un[:], vn[:, columns[piece]], start=(piece >= COSINE_FROM), stop=(piece < COSINE_FROM))
 
         def window():
             inv_total = held.tile([PREDS, 1], F32, name="inv_total")
             nc.vector.reciprocal(inv_total[:], total[:])
             nc.vector.tensor_scalar(neg_prob[:], expd[:], inv_total[:], -1.0, ALU.mult, ALU.mult)
 
-        def direction_cost():
-            nc.scalar.add(turn[:], neg_cos[:], 1.0)
+        def finish(piece):
+            cols = columns[piece]
+            nc.scalar.add(two_costs[:, cols], cost_ps[piece][:], 1.0)
+            picked = neg_prob[:].indirect(offsets[:, cols.start // 16 : cols.stop // 16])
+            nc.vector.tensor_tensor(cost[:, cols], picked, two_costs[:, cols], ALU.add)
+            nc.sync.dma_start(out[:, cols], cost[:, cols])
 
-        def look_up():
-            for first in range(0, TARGETS, CLASSES):
-                picked = neg_prob[:].indirect(offsets[:, first // 16 : (first + CLASSES) // 16])
-                nc.vector.tensor_tensor(two_costs[:, first : first + CLASSES], picked, turn[:, first : first + CLASSES], ALU.add)
-            for piece, cols in enumerate(columns):
-                nc.tensor.matmul(cost_ps[piece][:], ident[:], two_costs[:, cols], start=(piece > LOOK_UP_IN), stop=(piece < LOOK_UP_IN))
-
-        units = [(piece, duo) for piece in range(N_PIECES) for duo in range(POINTS // DUO)]
-        for u, (piece, duo) in enumerate(units):
-            cols, width = columns[piece], PIECE_WIDTHS[piece]
-            gaps = gap_pool.tile([PREDS, COORDS, DUO, POINTS, width], BF16, name="gaps")
-            for i in range(DUO):
-                for a in range(COORDS):
-                    k = COORDS * (DUO * duo + i) + a
-                    if k in (FIRST_SHARE if piece == 0 else LATER_SHARE):
-                        below = diff_pool.tile([PREDS, POINTS, width], BF16, name="below")
-                        nc.vector.tensor_scalar(below[:], y_all[:, a, :, cols], -1.0, x[:, k : k + 1], ALU.mult, ALU.add)
-                        nc.vector.scalar_tensor_tensor(gaps[:, a, i], y_all[:, a, :, cols], x[:, k : k + 1], below[:], ALU.subtract, ALU.max)
-                    else:
-                        nc.scalar.activation(gaps[:, a, i], y_all[:, a, :, cols], FUNC.Abs, bias=x[:, k : k + 1], scale=-1.0)
-            dist = dist_pool.tile([PREDS, DUO, POINTS, width], BF16, name="dist")
-            nc.vector.tensor_tensor(dist[:], gaps[:, 0], gaps[:, 1], ALU.add)
-            lower = dist_pool.tile([PREDS, POINTS, width], BF16, name="lower")
-            nc.vector.tensor_tensor(lower[:], dist[:, 0], dist[:, 1], ALU.min)
-            if duo == 0:
-                lower_before = lower
-            else:
-                near_pred = dist_pool.tile([PREDS, POINTS, width], BF16, name="near_pred")
-                nc.vector.tensor_tensor(near_pred[:], lower_before[:], lower[:], ALU.min)
-                for q in range(POINTS):
-                    nc.tensor.matmul(cost_ps[piece][:], eighth[:], near_pred[:, q], start=False, stop=False)
-            pair = dist_pool.tile([PREDS, DUO, 2, width], BF16, name="pair")
-            nc.vector.tensor_tensor(pair[:], dist[:, :, 0:2], dist[:, :, 2:4], ALU.min)
-            near_tgt = dist_pool.tile([PREDS, DUO, width], BF16, name="near_tgt")
-            nc.vector.tensor_tensor(near_tgt[:], pair[:, :, 0], pair[:, :, 1], ALU.min)
-            for i in range(DUO):
-                nc.tensor.matmul(cost_ps[piece][:], eighth[:], near_tgt[:, i], start=(piece <= LOOK_UP_IN and duo == 0 and i == 0), stop=(piece >= LOOK_UP_IN and duo == 1 and i == DUO - 1))
-            if u == 0:
-                unit_directions()
-            if u == 2:
-                exponentials()
-            if u == 3:
-                cosines()
-                window()
-            if u == 5:
-                direction_cost()
-            if piece == LOOK_UP_IN and duo == 0:
-                look_up()
-
-        cost = held.tile([PREDS, TARGETS], F32, name="cost")
+        unit_directions()
+        cost_ps = []
         for piece, cols in enumerate(columns):
-            nc.scalar.copy(cost[:, cols], cost_ps[piece][:])
-            if piece == N_PIECES - 2:
-                nc.sync.dma_start(out[:, 0 : cols.stop], cost[:, 0 : cols.stop])
-        nc.sync.dma_start(out[:, columns[-1]], cost[:, columns[-1]])
+            width = PIECE_WIDTHS[piece]
+            gaps = gap_pool.tile([PREDS, COORDS, POINTS, POINTS, width], BF16, name="gaps")
+            near = dist_pool.tile([PREDS, 2, HALF, HALF, width], BF16, name="near")
+            far = far_pool.tile([PREDS, 2, HALF, HALF, width], BF16, name="far", tag="far")
+            cost_ps.append(sums.tile([PREDS, width], F32, name="sum_ps"))
+            if piece >= COSINE_FROM:
+                cosine(piece)
+            for half in range(2):
+                ps = slice(HALF * half, HALF * half + HALF)
+                others = slice(HALF * (1 - half), HALF * (1 - half) + HALF)
+                share = [p for p in (FIRST_SHARE if piece == 0 else LATER_SHARE) if p in range(ps.start, ps.stop)]
+                for p in range(ps.start, ps.stop):
+                    for a in range(COORDS):
+                        if a == 0 or p not in share:
+                            bias = x[:, COORDS * p + a : COORDS * p + a + 1]
+                            nc.scalar.activation(gaps[:, a, p], y_all[:, a, :, cols], FUNC.Abs, bias=bias, scale=-1.0)
+                if share:
+                    lift = lift_pool.tile([PREDS, len(share), POINTS, width], BF16, name="lift")
+                    for i, p in enumerate(share):
+                        bias = x[:, COORDS * p + 1 : COORDS * p + 2]
+                        nc.vector.tensor_scalar(gaps[:, 1, p], y_all[:, 1, :, cols], -1.0, bias, ALU.mult, ALU.add)
+                        nc.vector.tensor_scalar(lift[:, i], gaps[:, 1, p], -2.0, 0.0, ALU.mult, ALU.max)
+                    lifted = slice(share[0] - ps.start, share[-1] + 1 - ps.start)
+                for a in range(COORDS):
+                    nc.tensor.matmul(far[:, half], one[:], gaps[:, a, ps, others], start=(a == 0), stop=(a == COORDS - 1 and not share))
+                nc.vector.tensor_tensor(near[:, half], gaps[:, 0, ps, ps], gaps[:, 1, ps, ps], ALU.add)
+                if share:
+                    nc.tensor.matmul(far[:, half, lifted], one[:], lift[:, :, others], start=False, stop=True)
+                    nc.vector.tensor_tensor(near[:, half, lifted], near[:, half, lifted], lift[:, :, ps], ALU.add)
+                if half == 1:
+                    low_p = dist_pool.tile([PREDS, 2, HALF, HALF, width], BF16, name="low_p")
+                    nc.vector.tensor_tensor(low_p[:], far[:], near[:, ::-1], ALU.min)
+                    low_q = dist_pool.tile([PREDS, 2, HALF, HALF, width], BF16, name="low_q")
+                    nc.vector.tensor_tensor(low_q[:], far[:], near[:], ALU.min)
+                    near_pred = dist_pool.tile([PREDS, 2, HALF, width], BF16, name="near_pred")
+                    nc.vector.tensor_tensor(near_pred[:], low_p[:, :, 0], low_p[:, :, 1], ALU.min)
+                    near_tgt = dist_pool.tile([PREDS, 2, HALF, width], BF16, name="near_tgt")
+                    nc.vector.tensor_tensor(near_tgt[:], low_q[:, :, :, 0], low_q[:, :, :, 1], ALU.min)
+                    minima = [m[:, h, i] for m in (near_pred, near_tgt) for h in range(2) for i in range(HALF)]
+                    for i, minimum in enumerate(minima):
+                        nc.tensor.matmul(cost_ps[piece][:], eighth[:], minimum, start=(piece < COSINE_FROM and i == 0), stop=(piece >= COSINE_FROM and i == len(minima) - 1))
+                u = 2 * piece + half
+                if u == 1:
+                    top_logits()
+                if u == 2:
+                    exponentials()
+                    window()
+                if u == 4:
+                    flipped_directions()
+            if piece == COSINE_FROM - 1:
+                for through in range(COSINE_FROM):
+                    cosine(through)
+                finish(0)
+            elif piece == COSINE_FROM:
+                finish(1)
+                finish(2)
+        finish(N_PIECES - 2)
+        finish(N_PIECES - 1)

@@ -18,8 +18,7 @@ PIECE_WIDTHS = (128, 128, 128, 64, 64)
 N_PIECES = len(PIECE_WIDTHS)
 COSINE_FROM = 3
 HALF = POINTS // 2
-FIRST_SHARE = (0, 1)
-LATER_SHARE = (POINTS - 1,)
+VECTOR_POINTS = ((0, 1, 3), (1, 3), (3,), (), ())
 FOLD = TARGETS // PREDS
 N_DIRS = FOLD + 1
 
@@ -32,7 +31,7 @@ def tile_hungarianmatcher_kernel(tc, logits, pred_poly, tgt_poly, offs, out):
     columns = [slice(start, start + width) for start, width in zip(starts, PIECE_WIDTHS)]
     with (
         tc.tile_pool(name="held", bufs=1) as held,
-        tc.tile_pool(name="gap_pool", bufs=3) as gap_pool,
+        tc.tile_pool(name="gap_pool", bufs=N_PIECES) as gap_pool,
         tc.tile_pool(name="lift_pool", bufs=3) as lift_pool,
         tc.tile_pool(name="dist_pool", bufs=3) as dist_pool,
         tc.psum_pool(name="far_pool", bufs=3) as far_pool,
@@ -141,7 +140,7 @@ def tile_hungarianmatcher_kernel(tc, logits, pred_poly, tgt_poly, offs, out):
             for half in range(2):
                 ps = slice(HALF * half, HALF * half + HALF)
                 others = slice(HALF * (1 - half), HALF * (1 - half) + HALF)
-                share = [p for p in (FIRST_SHARE if piece == 0 else LATER_SHARE) if p in range(ps.start, ps.stop)]
+                share = [p for p in VECTOR_POINTS[piece] if p in range(ps.start, ps.stop)]
                 for p in range(ps.start, ps.stop):
                     for a in range(COORDS):
                         if a == 0 or p not in share:

@@ -49,16 +49,15 @@ def tile_hungarianmatcher_kernel(tc, logits, pred_poly, tgt_poly, offs, out):
             for a in range(COORDS):
                 source = y_by_coord[a, :, cols].unsqueeze(0).to_broadcast([PREDS, POINTS, PIECE_WIDTHS[piece]])
                 nc.sync.dma_start(y_all[:, a, :, cols], source)
-            if piece == 1:
+            if piece == 0:
                 nc.sync.dma_start(ends[:, 0], y_folded[0])
                 nc.sync.dma_start(ends[:, 1], y_folded[POINTS - 1])
+            if piece == 1:
                 nc.sync.dma_start(logit[:], logits)
                 nc.sync.dma_start(offsets[:], offs)
 
         root = held.tile([PREDS, N_DIRS], F32, name="root")
         nc.gpsimd.memset(root[:], 0.5)
-        minus_one = held.tile([PREDS, N_DIRS], F32, name="minus_one")
-        nc.gpsimd.memset(minus_one[:], -1.0)
         warm = held.tile([PREDS, N_DIRS], F32, name="warm")
         nc.scalar.activation(warm[:], root[:], FUNC.Exp)
         one = held.tile([PREDS, PREDS], BF16, name="one")
@@ -72,28 +71,23 @@ def tile_hungarianmatcher_kernel(tc, logits, pred_poly, tgt_poly, offs, out):
         neg_un = held.tile([COORDS, PREDS], F32, name="neg_un")
         vn = held.tile([COORDS, TARGETS], F32, name="vn")
         expd = held.tile([PREDS, CLASSES], F32, name="expd")
-        total = held.tile([PREDS, 1], F32, name="total")
         neg_prob = held.tile([PREDS, CLASSES], F32, name="neg_prob")
         two_costs = held.tile([PREDS, TARGETS], F32, name="two_costs")
         cost = held.tile([PREDS, TARGETS], F32, name="cost")
         dirs = held.tile([PREDS, COORDS, N_DIRS], F32, name="dirs")
         unit = held.tile([PREDS, COORDS, N_DIRS], F32, name="unit")
+        divisors = held.tile([PREDS, N_DIRS + 1], F32, name="divisors")
 
-        def unit_directions():
-            nc.gpsimd.tensor_sub(dirs[:, :, 0:FOLD], ends[:, 1], ends[:, 0])
-            nc.gpsimd.tensor_sub(dirs[:, :, FOLD], x[:, 0:COORDS], x[:, (POINTS - 1) * COORDS : POINTS * COORDS])
+        def directions():
+            nc.vector.tensor_sub(dirs[:, :, 0:FOLD], ends[:, 1], ends[:, 0])
+            nc.vector.tensor_sub(dirs[:, :, FOLD], x[:, 0:COORDS], x[:, (POINTS - 1) * COORDS : POINTS * COORDS])
             squares = held.tile([PREDS, COORDS, N_DIRS], F32, name="squares")
-            nc.gpsimd.tensor_mul(squares[:], dirs[:], dirs[:])
+            nc.vector.tensor_mul(squares[:], dirs[:], dirs[:])
             norm2 = held.tile([PREDS, N_DIRS], F32, name="norm2")
-            nc.gpsimd.tensor_add(norm2[:], squares[:, 0, :], squares[:, 1, :])
+            nc.vector.tensor_add(norm2[:], squares[:, 0, :], squares[:, 1, :])
             norm = held.tile([PREDS, N_DIRS], F32, name="norm")
             nc.gpsimd.tensor_tensor(norm[:], norm2[:], root[:], ALU.pow)
-            norm_eps = held.tile([PREDS, N_DIRS], F32, name="norm_eps")
-            nc.gpsimd.tensor_scalar_add(norm_eps[:], norm[:], EPS)
-            inv_norm = held.tile([PREDS, N_DIRS], F32, name="inv_norm")
-            nc.gpsimd.tensor_tensor(inv_norm[:], norm_eps[:], minus_one[:], ALU.pow)
-            for a in range(COORDS):
-                nc.gpsimd.tensor_mul(unit[:, a], dirs[:, a], inv_norm[:])
+            nc.gpsimd.tensor_scalar_add(divisors[:, 0:N_DIRS], norm[:], EPS)
 
         def top_logits():
             top = held.tile([PREDS, 1], F32, name="top")
@@ -110,15 +104,17 @@ def tile_hungarianmatcher_kernel(tc, logits, pred_poly, tgt_poly, offs, out):
             nc.scalar.copy(vn[:].rearrange("a (m i) -> a m i", i=FOLD), vn_ps[:].rearrange("a i m -> a m i"))
 
         def exponentials():
-            nc.scalar.activation(expd[:], logit[:], FUNC.Exp, bias=neg_top[:], scale=1.0, accum_out=total[:])
+            nc.scalar.activation(expd[:], logit[:], FUNC.Exp, bias=neg_top[:], scale=1.0, accum_out=divisors[:, N_DIRS:])
 
         def cosine(piece):
             nc.tensor.matmul(cost_ps[piece][:], neg_un[:], vn[:, columns[piece]], start=(piece >= COSINE_FROM), stop=(piece < COSINE_FROM))
 
-        def window():
-            inv_total = held.tile([PREDS, 1], F32, name="inv_total")
-            nc.vector.reciprocal(inv_total[:], total[:])
-            nc.vector.tensor_scalar(neg_prob[:], expd[:], inv_total[:], -1.0, ALU.mult, ALU.mult)
+        def unit_directions_and_window():
+            inverse = held.tile([PREDS, N_DIRS + 1], F32, name="inverse")
+            nc.vector.reciprocal(inverse[:], divisors[:])
+            inv_norm = inverse[:, 0:N_DIRS].unsqueeze(1).to_broadcast([PREDS, COORDS, N_DIRS])
+            nc.vector.tensor_mul(unit[:], dirs[:], inv_norm)
+            nc.vector.tensor_scalar(neg_prob[:], expd[:], inverse[:, N_DIRS:], -1.0, ALU.mult, ALU.mult)
 
         def finish(piece):
             cols = columns[piece]
@@ -127,7 +123,7 @@ def tile_hungarianmatcher_kernel(tc, logits, pred_poly, tgt_poly, offs, out):
             nc.vector.tensor_tensor(cost[:, cols], picked, two_costs[:, cols], ALU.add)
             nc.sync.dma_start(out[:, cols], cost[:, cols])
 
-        unit_directions()
+        directions()
         cost_ps = []
         for piece, cols in enumerate(columns):
             width = PIECE_WIDTHS[piece]
@@ -176,7 +172,7 @@ def tile_hungarianmatcher_kernel(tc, logits, pred_poly, tgt_poly, offs, out):
                     top_logits()
                 if u == 2:
                     exponentials()
-                    window()
+                    unit_directions_and_window()
                 if u == 4:
                     flipped_directions()
             if piece == COSINE_FROM - 1:

@@ -16,6 +16,7 @@ COORDS = 2
 EPS = 1e-6
 PIECE_WIDTHS = (128, 128, 128, 64, 64)
 N_PIECES = len(PIECE_WIDTHS)
+Y_LOADS = (slice(0, 128), slice(128, 256), slice(256, TARGETS))
 COSINE_FROM = 3
 HALF = POINTS // 2
 VECTOR_POINTS = ((0, 1, 3), (1, 3), (3,), (), ())
@@ -45,14 +46,13 @@ def tile_hungarianmatcher_kernel(tc, logits, pred_poly, tgt_poly, offs, out):
         logit = held.tile([PREDS, CLASSES], F32, name="logit")
         offsets = held.tile([PREDS, TARGETS // 16], U16, name="offsets")
         nc.sync.dma_start(x[:], pred_poly)
-        for piece, cols in enumerate(columns):
+        for group, cols in enumerate(Y_LOADS):
             for a in range(COORDS):
-                source = y_by_coord[a, :, cols].unsqueeze(0).to_broadcast([PREDS, POINTS, PIECE_WIDTHS[piece]])
+                source = y_by_coord[a, :, cols].unsqueeze(0).to_broadcast([PREDS, POINTS, cols.stop - cols.start])
                 nc.sync.dma_start(y_all[:, a, :, cols], source)
-            if piece == 0:
+            if group == 1:
                 nc.sync.dma_start(ends[:, 0], y_folded[0])
                 nc.sync.dma_start(ends[:, 1], y_folded[POINTS - 1])
-            if piece == 1:
                 nc.sync.dma_start(logit[:], logits)
                 nc.sync.dma_start(offsets[:], offs)
 

import concourse.mybir as mybir
from concourse.masks import make_identity

F32 = mybir.dt.float32
BF16 = mybir.dt.bfloat16
U16 = mybir.dt.uint16
ALU = mybir.AluOpType
FUNC = mybir.ActivationFunctionType
FREE = mybir.AxisListType.X

PREDS = 128
CLASSES = 256
TARGETS = 512
POINTS = 4
COORDS = 2
EPS = 1e-6
PIECE_WIDTHS = (128, 128, 128, 64, 64)
N_PIECES = len(PIECE_WIDTHS)
Y_LOADS = (slice(0, 128), slice(128, 256), slice(256, TARGETS))
COSINE_FROM = 3
HALF = POINTS // 2
VECTOR_POINTS = ((0, 1, 3), (1, 3), (3,), (), ())
FOLD = TARGETS // PREDS
N_DIRS = FOLD + 1

FLOPS = PREDS * TARGETS * 118


def tile_hungarianmatcher_kernel(tc, logits, pred_poly, tgt_poly, offs, out):
    nc = tc.nc
    starts = [sum(PIECE_WIDTHS[:piece]) for piece in range(N_PIECES)]
    columns = [slice(start, start + width) for start, width in zip(starts, PIECE_WIDTHS)]
    with (
        tc.tile_pool(name="held", bufs=1) as held,
        tc.tile_pool(name="gap_pool", bufs=N_PIECES) as gap_pool,
        tc.tile_pool(name="lift_pool", bufs=3) as lift_pool,
        tc.tile_pool(name="dist_pool", bufs=3) as dist_pool,
        tc.psum_pool(name="far_pool", bufs=3) as far_pool,
        tc.psum_pool(name="sums", bufs=4) as sums,
    ):
        x = held.tile([PREDS, POINTS * COORDS], F32, name="x")
        ends = held.tile([PREDS, 2, COORDS, FOLD], F32, name="ends")
        y_folded = tgt_poly.rearrange("(q a) (m i) -> q m a i", a=COORDS, i=FOLD)
        y_all = held.tile([PREDS, COORDS, POINTS, TARGETS], F32, name="y_all")
        y_by_coord = tgt_poly.rearrange("(q a) j -> a q j", a=COORDS)
        logit = held.tile([PREDS, CLASSES], F32, name="logit")
        offsets = held.tile([PREDS, TARGETS // 16], U16, name="offsets")
        nc.sync.dma_start(x[:], pred_poly)
        for group, cols in enumerate(Y_LOADS):
            for a in range(COORDS):
                source = y_by_coord[a, :, cols].unsqueeze(0).to_broadcast([PREDS, POINTS, cols.stop - cols.start])
                nc.sync.dma_start(y_all[:, a, :, cols], source)
            if group == 1:
                nc.sync.dma_start(ends[:, 0], y_folded[0])
                nc.sync.dma_start(ends[:, 1], y_folded[POINTS - 1])
                nc.sync.dma_start(logit[:], logits)
                nc.sync.dma_start(offsets[:], offs)

        root = held.tile([PREDS, N_DIRS], F32, name="root")
        nc.gpsimd.memset(root[:], 0.5)
        warm = held.tile([PREDS, N_DIRS], F32, name="warm")
        nc.scalar.activation(warm[:], root[:], FUNC.Exp)
        one = held.tile([PREDS, PREDS], BF16, name="one")
        make_identity(nc, one[:])
        eighth = held.tile([PREDS, PREDS], BF16, name="eighth")
        nc.gpsimd.tensor_scalar_mul(eighth[:], one[:], 1.0 / (2 * POINTS))
        ident = held.tile([PREDS, PREDS], F32, name="ident")
        make_identity(nc, ident[:])

        neg_top = held.tile([PREDS, 1], F32, name="neg_top")
        neg_un = held.tile([COORDS, PREDS], F32, name="neg_un")
        vn = held.tile([COORDS, TARGETS], F32, name="vn")
        expd = held.tile([PREDS, CLASSES], F32, name="expd")
        neg_prob = held.tile([PREDS, CLASSES], F32, name="neg_prob")
        two_costs = held.tile([PREDS, TARGETS], F32, name="two_costs")
        cost = held.tile([PREDS, TARGETS], F32, name="cost")
        dirs = held.tile([PREDS, COORDS, N_DIRS], F32, name="dirs")
        unit = held.tile([PREDS, COORDS, N_DIRS], F32, name="unit")
        divisors = held.tile([PREDS, N_DIRS + 1], F32, name="divisors")

        def directions():
            nc.vector.tensor_sub(dirs[:, :, 0:FOLD], ends[:, 1], ends[:, 0])
            nc.vector.tensor_sub(dirs[:, :, FOLD], x[:, 0:COORDS], x[:, (POINTS - 1) * COORDS : POINTS * COORDS])
            squares = held.tile([PREDS, COORDS, N_DIRS], F32, name="squares")
            nc.vector.tensor_mul(squares[:], dirs[:], dirs[:])
            norm2 = held.tile([PREDS, N_DIRS], F32, name="norm2")
            nc.vector.tensor_add(norm2[:], squares[:, 0, :], squares[:, 1, :])
            norm = held.tile([PREDS, N_DIRS], F32, name="norm")
            nc.gpsimd.tensor_tensor(norm[:], norm2[:], root[:], ALU.pow)
            nc.gpsimd.tensor_scalar_add(divisors[:, 0:N_DIRS], norm[:], EPS)

        def top_logits():
            top = held.tile([PREDS, 1], F32, name="top")
            nc.vector.reduce_max(top[:], logit[:], axis=FREE)
            nc.gpsimd.tensor_scalar_mul(neg_top[:], top[:], -1.0)

        def flipped_directions():
            vn_ps = far_pool.tile([COORDS, FOLD, PREDS], F32, name="vn_ps", tag="far")
            un_ps = far_pool.tile([COORDS, PREDS], F32, name="un_ps", tag="far")
            for i in range(FOLD):
                nc.tensor.transpose(vn_ps[:, i, :], unit[:, :, i], ident[:])
            nc.tensor.transpose(un_ps[:], unit[:, :, FOLD], ident[:])
            nc.scalar.copy(neg_un[:], un_ps[:])
            nc.scalar.copy(vn[:].rearrange("a (m i) -> a m i", i=FOLD), vn_ps[:].rearrange("a i m -> a m i"))

        def exponentials():
            nc.scalar.activation(expd[:], logit[:], FUNC.Exp, bias=neg_top[:], scale=1.0, accum_out=divisors[:, N_DIRS:])

        def cosine(piece):
            nc.tensor.matmul(cost_ps[piece][:], neg_un[:], vn[:, columns[piece]], start=(piece >= COSINE_FROM), stop=(piece < COSINE_FROM))

        def unit_directions_and_window():
            inverse = held.tile([PREDS, N_DIRS + 1], F32, name="inverse")
            nc.vector.reciprocal(inverse[:], divisors[:])
            inv_norm = inverse[:, 0:N_DIRS].unsqueeze(1).to_broadcast([PREDS, COORDS, N_DIRS])
            nc.vector.tensor_mul(unit[:], dirs[:], inv_norm)
            nc.vector.tensor_scalar(neg_prob[:], expd[:], inverse[:, N_DIRS:], -1.0, ALU.mult, ALU.mult)

        def finish(piece):
            cols = columns[piece]
            nc.scalar.add(two_costs[:, cols], cost_ps[piece][:], 1.0)
            picked = neg_prob[:].indirect(offsets[:, cols.start // 16 : cols.stop // 16])
            nc.vector.tensor_tensor(cost[:, cols], picked, two_costs[:, cols], ALU.add)
            nc.sync.dma_start(out[:, cols], cost[:, cols])

        directions()
        cost_ps = []
        for piece, cols in enumerate(columns):
            width = PIECE_WIDTHS[piece]
            gaps = gap_pool.tile([PREDS, COORDS, POINTS, POINTS, width], BF16, name="gaps")
            near = dist_pool.tile([PREDS, 2, HALF, HALF, width], BF16, name="near")
            far = far_pool.tile([PREDS, 2, HALF, HALF, width], BF16, name="far", tag="far")
            cost_ps.append(sums.tile([PREDS, width], F32, name="sum_ps"))
            if piece >= COSINE_FROM:
                cosine(piece)
            for half in range(2):
                ps = slice(HALF * half, HALF * half + HALF)
                others = slice(HALF * (1 - half), HALF * (1 - half) + HALF)
                share = [p for p in VECTOR_POINTS[piece] if p in range(ps.start, ps.stop)]
                for p in range(ps.start, ps.stop):
                    for a in range(COORDS):
                        if a == 0 or p not in share:
                            bias = x[:, COORDS * p + a : COORDS * p + a + 1]
                            nc.scalar.activation(gaps[:, a, p], y_all[:, a, :, cols], FUNC.Abs, bias=bias, scale=-1.0)
                if share:
                    lift = lift_pool.tile([PREDS, len(share), POINTS, width], BF16, name="lift")
                    for i, p in enumerate(share):
                        bias = x[:, COORDS * p + 1 : COORDS * p + 2]
                        nc.vector.tensor_scalar(gaps[:, 1, p], y_all[:, 1, :, cols], -1.0, bias, ALU.mult, ALU.add)
                        nc.vector.tensor_scalar(lift[:, i], gaps[:, 1, p], -2.0, 0.0, ALU.mult, ALU.max)
                    lifted = slice(share[0] - ps.start, share[-1] + 1 - ps.start)
                for a in range(COORDS):
                    nc.tensor.matmul(far[:, half], one[:], gaps[:, a, ps, others], start=(a == 0), stop=(a == COORDS - 1 and not share))
                nc.vector.tensor_tensor(near[:, half], gaps[:, 0, ps, ps], gaps[:, 1, ps, ps], ALU.add)
                if share:
                    nc.tensor.matmul(far[:, half, lifted], one[:], lift[:, :, others], start=False, stop=True)
                    nc.vector.tensor_tensor(near[:, half, lifted], near[:, half, lifted], lift[:, :, ps], ALU.add)
                if half == 1:
                    low_p = dist_pool.tile([PREDS, 2, HALF, HALF, width], BF16, name="low_p")
                    nc.vector.tensor_tensor(low_p[:], far[:], near[:, ::-1], ALU.min)
                    low_q = dist_pool.tile([PREDS, 2, HALF, HALF, width], BF16, name="low_q")
                    nc.vector.tensor_tensor(low_q[:], far[:], near[:], ALU.min)
                    near_pred = dist_pool.tile([PREDS, 2, HALF, width], BF16, name="near_pred")
                    nc.vector.tensor_tensor(near_pred[:], low_p[:, :, 0], low_p[:, :, 1], ALU.min)
                    near_tgt = dist_pool.tile([PREDS, 2, HALF, width], BF16, name="near_tgt")
                    nc.vector.tensor_tensor(near_tgt[:], low_q[:, :, :, 0], low_q[:, :, :, 1], ALU.min)
                    minima = [m[:, h, i] for m in (near_pred, near_tgt) for h in range(2) for i in range(HALF)]
                    for i, minimum in enumerate(minima):
                        nc.tensor.matmul(cost_ps[piece][:], eighth[:], minimum, start=(piece < COSINE_FROM and i == 0), stop=(piece >= COSINE_FROM and i == len(minima) - 1))
                u = 2 * piece + half
                if u == 1:
                    top_logits()
                if u == 2:
                    exponentials()
                    unit_directions_and_window()
                if u == 4:
                    flipped_directions()
            if piece == COSINE_FROM - 1:
                for through in range(COSINE_FROM):
                    cosine(through)
                finish(0)
            elif piece == COSINE_FROM:
                finish(1)
                finish(2)
        finish(N_PIECES - 2)
        finish(N_PIECES - 1)
